import numpy as np
import ml_dtypes


def mxq(x, axis, fmt="e4m3"):
    dtype, down = {"e4m3": (ml_dtypes.float8_e4m3fn, 7), "e5m2": (ml_dtypes.float8_e5m2, 14)}[fmt]
    v = np.moveaxis(np.asarray(x, np.float32).astype(ml_dtypes.bfloat16).astype(np.float64), axis, -1)
    blocks = v.reshape(v.shape[:-1] + (-1, 32))
    amax = np.abs(blocks).max(-1, keepdims=True)
    byte = np.maximum(np.where(amax > 0, np.frexp(amax)[1] - 1 + 127, 0) - down, 1)
    scale = np.exp2(byte - 127.0)
    codes = (blocks / scale).astype(np.float32).astype(dtype).astype(np.float64)
    return np.moveaxis((codes * scale).reshape(v.shape), -1, axis)


WIDE = False


def mx_kscale(k):
    if not WIDE:
        return np.ones(k)
    levels = np.array([10, -10, 5, -5, 0])
    a = np.random.permutation(np.resize(levels, k // 512 * 4)).reshape(k // 512, 4)
    idx = np.arange(k)
    return np.exp2(a[idx // 512, idx % 128 // 32])


BF16 = ml_dtypes.bfloat16


def bf(x):
    return np.asarray(x, np.float32).astype(BF16)


def f64(x):
    return np.asarray(x).astype(np.float64)


E2M1 = np.array([0.0, 0.5, 1.0, 1.5, 2.0, 3.0, 4.0, 6.0, -0.0, -0.5, -1.0, -1.5, -2.0, -3.0, -4.0, -6.0])


def pack_weight(w, fmt):
    k, n = w.shape
    w = f64(bf(w)).reshape(k // 32, 32, n)
    amax = np.abs(w).max(1)
    if fmt == "e4m3":
        byte = np.frexp(amax)[1] - 1 + 127 - 7
    else:
        mant, ex = np.frexp(amax / 6.0)
        byte = np.where(mant > 0.5, ex, ex - 1) + 127
    byte = np.clip(np.where(amax > 0, byte, 1), 1, 254)
    scaled = (w * np.exp2(127.0 - byte)[:, None, :]).reshape(k, n).astype(np.float32)
    by_word = np.ascontiguousarray(scaled.reshape(k // 512, 128, 4, n).transpose(0, 1, 3, 2))
    if fmt == "e4m3":
        words = by_word.astype(ml_dtypes.float8_e4m3fn).view(np.uint8)
    else:
        c = by_word.astype(ml_dtypes.float4_e2m1fn).view(np.uint8) & 0xF
        words = c[..., 0::2] | (c[..., 1::2] << 4)
    return np.ascontiguousarray(words), np.ascontiguousarray(byte.astype(np.uint8).reshape(k // 512, 16, n))


def unpack_weight(words, scales, fmt):
    g, p, n, _ = words.shape
    if fmt == "e4m3":
        vals = np.ascontiguousarray(words).view(ml_dtypes.float8_e4m3fn).astype(np.float64)
    else:
        nib = np.empty((g, p, n, 4), np.uint8)
        nib[..., 0::2] = words & 0xF
        nib[..., 1::2] = words >> 4
        vals = E2M1[nib]
    vals = vals * np.repeat(np.exp2(scales.astype(np.float64) - 127.0), 8, axis=1)[..., None]
    return vals.transpose(0, 1, 3, 2).reshape(g * 512, n)


B, I, O = 4096, 1024, 128
DEGREE = 3
KNOTS = (0.2, 0.4, 0.6, 0.8)
SDIM = DEGREE + 1 + len(KNOTS)
T_MAX = 2.0


def truncated_power_basis(t):
    cols = [np.ones_like(t)]
    for p in range(1, DEGREE + 1):
        cols.append(t ** p)
    for c in KNOTS:
        cols.append(np.maximum(t - c, 0.0) ** DEGREE)
    return np.stack(cols, axis=1)


def setup_inputs():
    s = mx_kscale(I)
    t = np.random.random((B, 1)) * T_MAX
    x = np.random.random((B, I)) * s
    w = np.random.standard_normal((SDIM, I, O)) * (0.52 / np.sqrt(I)) / s[None, :, None]
    words, scales = pack_weight(w.reshape(-1, O), "e4m3")
    return {"inputs": bf(np.concatenate([t, x], axis=1)), "W_wts_words": words, "W_wts_scales": scales,
            "b_wts": bf(np.random.standard_normal((SDIM, O)) * 0.3)}


def reference(inputs, W_wts_words, W_wts_scales, b_wts):
    inputs = f64(inputs)
    treatment = inputs[:, 0]
    features = inputs[:, 1:]
    basis = truncated_power_basis(treatment)
    Wk = unpack_weight(W_wts_words, W_wts_scales, "e4m3").reshape(SDIM, I, O)
    P = mxq(features, 1, "e4m3") @ Wk
    out = (basis.T[:, :, None] * P).sum(0)
    out = out + (basis[:, :, None] * f64(b_wts)[None, :, :]).sum(1)
    return out

@@ -1,0 +1,232 @@
+from contextlib import ExitStack
+
+import concourse.mybir as mybir
+from concourse.masks import make_identity
+
+F32 = mybir.dt.float32
+BF16 = mybir.dt.bfloat16
+I32 = mybir.dt.int32
+U32 = mybir.dt.uint32
+U8 = mybir.dt.uint8
+FP8X4 = mybir.dt.float8_e4m3fn_x4
+ALU = mybir.AluOpType
+
+P = 128
+BATCH, FEATURES, OUTS, TERMS = 4096, 1024, 128, 8
+KNOTS = (0.2, 0.4, 0.6, 0.8)
+FLOPS = 2 * BATCH * FEATURES * TERMS * OUTS
+
+PACK = 4
+K_PASS = P * PACK
+PASSES = FEATURES // K_PASS
+HALF_WORDS = 2
+N_MOVE = 512
+BANKS = TERMS * OUTS // N_MOVE
+TERMS_PER_BANK = TERMS // BANKS
+
+SLOTS = BATCH // P
+PAIR = 2
+N_PAIRS = SLOTS // PAIR
+ROW_PITCH = 1040
+X_AT = 16
+T_AT = X_AT - 1
+
+
+def tile_vclinear_t_e_kernel(tc, inputs, W_wts_words, W_wts_scales, b_wts, out):
+    nc = tc.nc
+    with ExitStack() as ctx:
+        ctx.enter_context(tc.manual_schedule())
+        keep = ctx.enter_context(tc.tile_pool(name="keep", bufs=1))
+        stage = ctx.enter_context(tc.tile_pool(name="stage", bufs=3))
+        psum_xt = ctx.enter_context(tc.psum_pool(name="psum_xt", bufs=PAIR))
+        psum_prod = ctx.enter_context(tc.psum_pool(name="psum_prod", bufs=PAIR * BANKS))
+        psum_bias = ctx.enter_context(tc.psum_pool(name="psum_bias", bufs=2))
+
+        ident = keep.tile([P, P], F32)
+        x_rows = keep.tile([P, SLOTS, ROW_PITCH], BF16, align_bytes=64)
+        w_codes = keep.tile([P, PASSES, TERMS * OUTS], U32, align_bytes=64)
+        w_scales = keep.tile([P, PASSES, TERMS * OUTS], U8, align_bytes=64)
+        scale_rows = keep.tile([P, TERMS * PASSES * OUTS], U8, align_bytes=64)
+        bias_w_bf = keep.tile([P, PAIR, OUTS], BF16)
+        bias_w = keep.tile([P, PAIR, OUTS], F32)
+        basis = keep.tile([P, N_PAIRS, P], F32)
+        out_rows = keep.tile([P, SLOTS, OUTS], F32)
+
+        make_identity(nc, ident[:])
+        nc.vector.memset(bias_w_bf[:], 0.0)
+        nc.vector.memset(scale_rows[:].bitcast(I32), 0)
+        nc.vector.memset(basis[:], 0.0)
+        nc.gpsimd.memset(basis[:, :, 0 : PAIR * TERMS : TERMS], 1.0)
+
+        for i in range(PAIR):
+            nc.sync.dma_start(out=bias_w_bf[TERMS * i : TERMS * (i + 1), i, :], in_=b_wts)
+
+        rows_dram = inputs.rearrange("(p j) c -> p j c", j=SLOTS)
+
+        def load_pair(n):
+            slots = slice(PAIR * n, PAIR * (n + 1))
+            nc.sync.dma_start(out=x_rows[:, slots, T_AT:ROW_PITCH], in_=rows_dram[:, slots, :])
+
+        load_pair(0)
+        load_pair(1)
+        scales_dram = W_wts_scales.bitcast(I32).rearrange("a (q r) n -> q r a n", r=4)
+        for Q in range(4):
+            nc.sync.dma_start(
+                out=scale_rows[32 * Q : 32 * Q + 4, :]
+                .bitcast(I32)
+                .rearrange("r (a n) -> r a n", a=TERMS * PASSES),
+                in_=scales_dram[Q],
+            )
+        words_dram = (
+            W_wts_words.rearrange("a p n t -> a p (n t)")
+            .bitcast(I32)
+            .rearrange("(s g) p n -> g p s n", g=PASSES)
+        )
+        for g in range(PASSES):
+            nc.sync.dma_start(
+                out=w_codes[:, g, :].bitcast(I32).rearrange("p (s n) -> p s n", s=TERMS),
+                in_=words_dram[g],
+            )
+        for n in range(2, N_PAIRS):
+            load_pair(n)
+
+        nc.vector.tensor_copy(out=bias_w[:], in_=bias_w_bf[:])
+        nc.vector.tensor_copy(
+            out=w_scales[:]
+            .rearrange("p g c -> p (g c)")
+            .bitcast(I32)
+            .rearrange("p (g s n) -> p g s n", g=PASSES, s=TERMS),
+            in_=scale_rows[:].bitcast(I32).rearrange("p (s g n) -> p g s n", g=PASSES, s=TERMS),
+        )
+
+        def spline_basis(n):
+            fn = basis[:, n, 0 : PAIR * TERMS].rearrange("p (i s) -> p i s", s=TERMS)
+            hinge = stage.tile([P, PAIR, len(KNOTS)], F32)
+            hinge_sq = stage.tile([P, PAIR, len(KNOTS)], F32)
+            nc.gpsimd.tensor_copy(out=fn[:, :, 1], in_=x_rows[:, PAIR * n : PAIR * (n + 1), T_AT])
+            nc.gpsimd.tensor_mul(out=fn[:, :, 2], in0=fn[:, :, 1], in1=fn[:, :, 1])
+            nc.gpsimd.tensor_mul(out=fn[:, :, 3], in0=fn[:, :, 2], in1=fn[:, :, 1])
+            for c, knot in enumerate(KNOTS):
+                nc.gpsimd.tensor_scalar(
+                    out=hinge[:, :, c],
+                    in0=fn[:, :, 1],
+                    scalar1=knot,
+                    scalar2=0.0,
+                    op0=ALU.subtract,
+                    op1=ALU.max,
+                )
+            nc.gpsimd.tensor_mul(out=hinge_sq[:], in0=hinge[:], in1=hinge[:])
+            nc.gpsimd.tensor_mul(out=fn[:, :, 4:TERMS], in0=hinge_sq[:], in1=hinge[:])
+
+        def transpose_features(n):
+            grouped = stage.tile([P, PAIR, PASSES, P, PACK], BF16, align_bytes=64)
+            for i in range(PAIR):
+                words = x_rows[:, PAIR * n + i, X_AT:ROW_PITCH].bitcast(F32)
+                xt = psum_xt.tile([P, PASSES, HALF_WORDS, P], F32)
+                for g in range(PASSES):
+                    for u in range(HALF_WORDS):
+                        first = g * P * HALF_WORDS + u
+                        nc.tensor.transpose(
+                            xt[:, g, u, :],
+                            words[:, first : (g + 1) * P * HALF_WORDS : HALF_WORDS],
+                            ident[:],
+                        )
+                nc.scalar.copy(
+                    out=grouped[:, i].bitcast(F32), in_=xt[:].rearrange("p g u b -> p g b u")
+                )
+            return grouped
+
+        def quantise(grouped):
+            x_codes = stage.tile([P, PAIR * PASSES * P], U32, align_bytes=64)
+            x_scales = stage.tile([P, PAIR * PASSES * P], U8, align_bytes=64)
+            nc.vector.quantize_mx(
+                out=x_codes[:].bitcast(FP8X4),
+                scales=x_scales[:],
+                in_=grouped[:].rearrange("p i g b t -> p (i g b t)"),
+            )
+            return x_codes, x_scales
+
+        def transpose_basis(n):
+            bias_ps = psum_bias.tile([P, (1 + PAIR) * P], F32)
+            basis_t = stage.tile([P, P], F32)
+            nc.tensor.transpose(bias_ps[:, 0:P], basis[:, n, :], ident[:])
+            nc.scalar.copy(out=basis_t[:], in_=bias_ps[:, 0:P])
+            return bias_ps, basis_t
+
+        def bias_term(bias_ps, basis_t):
+            bias_sb = stage.tile([P, PAIR, OUTS], F32)
+            for i in range(PAIR):
+                nc.tensor.matmul(
+                    bias_ps[:, (1 + i) * P : (2 + i) * P],
+                    lhsT=basis_t[:],
+                    rhs=bias_w[:, i, :],
+                    start=True,
+                    stop=True,
+                )
+            nc.scalar.copy(
+                out=bias_sb[:].rearrange("p i o -> p (i o)"), in_=bias_ps[:, P : (1 + PAIR) * P]
+            )
+            return bias_sb
+
+        def multiply(x_codes, x_scales):
+            products = []
+            for i in range(PAIR):
+                for h in range(BANKS):
+                    prod = psum_prod.tile([P, N_MOVE], F32)
+                    for g in range(PASSES):
+                        rows = slice((i * PASSES + g) * P, (i * PASSES + g + 1) * P)
+                        cols = slice(h * N_MOVE, (h + 1) * N_MOVE)
+                        nc.tensor.matmul_mx(
+                            out=prod[:],
+                            lhsT=x_codes[:, rows].bitcast(FP8X4),
+                            lhsT_scale=x_scales[:, rows],
+                            rhs=w_codes[:, g, cols].bitcast(FP8X4),
+                            rhs_scale=w_scales[:, g, cols],
+                            start=(g == 0),
+                            stop=(g == PASSES - 1),
+                        )
+                    products.append(prod)
+            return products
+
+        def combine(n, products, bias_sb):
+            for s in range(TERMS):
+                for i in range(PAIR):
+                    total = out_rows[:, PAIR * n + i, :]
+                    piece = products[i * BANKS + s // TERMS_PER_BANK][
+                        :, (s % TERMS_PER_BANK) * OUTS : (s % TERMS_PER_BANK + 1) * OUTS
+                    ]
+                    if s == 0:
+                        nc.vector.tensor_tensor(
+                            out=total, in0=piece, in1=bias_sb[:, i, :], op=ALU.add
+                        )
+                    else:
+                        nc.vector.scalar_tensor_tensor(
+                            out=total,
+                            in0=piece,
+                            scalar=basis[:, n, i * TERMS + s : i * TERMS + s + 1],
+                            in1=total,
+                            op0=ALU.mult,
+                            op1=ALU.add,
+                        )
+
+        out_dram = out.rearrange("(p j) o -> p j o", j=SLOTS)
+
+        def store(n):
+            slots = slice(PAIR * n, PAIR * (n + 1))
+            nc.sync.dma_start(out=out_dram[:, slots, :], in_=out_rows[:, slots, :])
+
+        spline_basis(0)
+        quantised = quantise(transpose_features(0))
+        bias_tiles = transpose_basis(0)
+        for n in range(N_PAIRS):
+            if n + 1 < N_PAIRS:
+                spline_basis(n + 1)
+                grouped_next = transpose_features(n + 1)
+                bias_tiles_next = transpose_basis(n + 1)
+            bias_sb = bias_term(*bias_tiles)
+            products = multiply(*quantised)
+            if n + 1 < N_PAIRS:
+                quantised = quantise(grouped_next)
+                bias_tiles = bias_tiles_next
+            combine(n, products, bias_sb)
+            store(n)

@@ -118,19 +118,23 @@ def tile_vclinear_t_e_kernel(tc, inputs, W_wts_words, W_wts_scales, b_wts, out):
             nc.gpsimd.tensor_mul(out=hinge_sq[:], in0=hinge[:], in1=hinge[:])
             nc.gpsimd.tensor_mul(out=fn[:, :, 4:TERMS], in0=hinge_sq[:], in1=hinge[:])
 
-        def transpose_features(n):
-            grouped = stage.tile([P, PAIR, PASSES, P, PACK], BF16, align_bytes=64)
+        def sort_words(n):
+            halves = stage.tile([P, PAIR, PASSES, HALF_WORDS, P], F32)
             for i in range(PAIR):
                 words = x_rows[:, PAIR * n + i, X_AT:ROW_PITCH].bitcast(F32)
+                nc.scalar.copy(
+                    out=halves[:, i],
+                    in_=words.rearrange("p (g c u) -> p g u c", g=PASSES, u=HALF_WORDS),
+                )
+            return halves
+
+        def transpose_features(halves):
+            grouped = stage.tile([P, PAIR, PASSES, P, PACK], BF16, align_bytes=64)
+            for i in range(PAIR):
                 xt = psum_xt.tile([P, PASSES, HALF_WORDS, P], F32)
                 for g in range(PASSES):
                     for u in range(HALF_WORDS):
-                        first = g * P * HALF_WORDS + u
-                        nc.tensor.transpose(
-                            xt[:, g, u, :],
-                            words[:, first : (g + 1) * P * HALF_WORDS : HALF_WORDS],
-                            ident[:],
-                        )
+                        nc.tensor.transpose(xt[:, g, u, :], halves[:, i, g, u, :], ident[:])
                 nc.scalar.copy(
                     out=grouped[:, i].bitcast(F32), in_=xt[:].rearrange("p g u b -> p g b u")
                 )
@@ -216,14 +220,18 @@ def tile_vclinear_t_e_kernel(tc, inputs, W_wts_words, W_wts_scales, b_wts, out):
             nc.sync.dma_start(out=out_dram[:, slots, :], in_=out_rows[:, slots, :])
 
         spline_basis(0)
-        quantised = quantise(transpose_features(0))
+        grouped_first = transpose_features(sort_words(0))
+        halves_next = sort_words(1)
+        quantised = quantise(grouped_first)
         bias_tiles = transpose_basis(0)
         for n in range(N_PAIRS):
             if n + 1 < N_PAIRS:
                 spline_basis(n + 1)
-                grouped_next = transpose_features(n + 1)
+                grouped_next = transpose_features(halves_next)
                 bias_tiles_next = transpose_basis(n + 1)
             bias_sb = bias_term(*bias_tiles)
+            if n + 2 < N_PAIRS:
+                halves_next = sort_words(n + 2)
             products = multiply(*quantised)
             if n + 1 < N_PAIRS:
                 quantised = quantise(grouped_next)

@@ -27,9 +27,13 @@ TERMS_PER_BANK = TERMS // BANKS
 SLOTS = BATCH // P
 PAIR = 2
 N_PAIRS = SLOTS // PAIR
+QUAD = 4
 ROW_PITCH = 1040
 X_AT = 16
 T_AT = X_AT - 1
+PARTS = 3
+PSUM_BANKS = 8
+PRODUCT_BANKS = PSUM_BANKS - PAIR - 1
 
 
 def tile_vclinear_t_e_kernel(tc, inputs, W_wts_words, W_wts_scales, b_wts, out):
@@ -39,27 +43,33 @@ def tile_vclinear_t_e_kernel(tc, inputs, W_wts_words, W_wts_scales, b_wts, out):
         keep = ctx.enter_context(tc.tile_pool(name="keep", bufs=1))
         stage = ctx.enter_context(tc.tile_pool(name="stage", bufs=3))
         psum_xt = ctx.enter_context(tc.psum_pool(name="psum_xt", bufs=PAIR))
-        psum_prod = ctx.enter_context(tc.psum_pool(name="psum_prod", bufs=PAIR * BANKS))
-        psum_bias = ctx.enter_context(tc.psum_pool(name="psum_bias", bufs=2))
+        psum_prod = ctx.enter_context(tc.psum_pool(name="psum_prod", bufs=PRODUCT_BANKS))
+        psum_small = ctx.enter_context(tc.psum_pool(name="psum_small", bufs=1))
 
         ident = keep.tile([P, P], F32)
+        ident_bf = keep.tile([P, P], BF16)
         x_rows = keep.tile([P, SLOTS, ROW_PITCH], BF16, align_bytes=64)
         w_codes = keep.tile([P, PASSES, TERMS * OUTS], U32, align_bytes=64)
         w_scales = keep.tile([P, PASSES, TERMS * OUTS], U8, align_bytes=64)
         scale_rows = keep.tile([P, TERMS * PASSES * OUTS], U8, align_bytes=64)
-        bias_w_bf = keep.tile([P, PAIR, OUTS], BF16)
-        bias_w = keep.tile([P, PAIR, OUTS], F32)
-        basis = keep.tile([P, N_PAIRS, P], F32)
+        bias_w = keep.tile([P, PAIR, OUTS], BF16)
+        basis = keep.tile([P, SLOTS, TERMS], F32)
+        basis_parts = keep.tile([P, N_PAIRS, P], BF16)
         out_rows = keep.tile([P, SLOTS, OUTS], F32)
 
         make_identity(nc, ident[:])
-        nc.vector.memset(bias_w_bf[:], 0.0)
+        make_identity(nc, ident_bf[:])
+        nc.vector.memset(bias_w[:], 0.0)
         nc.vector.memset(scale_rows[:].bitcast(I32), 0)
-        nc.vector.memset(basis[:], 0.0)
-        nc.gpsimd.memset(basis[:, :, 0 : PAIR * TERMS : TERMS], 1.0)
+        nc.vector.memset(basis_parts[:], 0.0)
+        nc.gpsimd.memset(basis[:, :, 0], 1.0)
 
         for i in range(PAIR):
-            nc.sync.dma_start(out=bias_w_bf[TERMS * i : TERMS * (i + 1), i, :], in_=b_wts)
+            rows = slice(PARTS * TERMS * i, PARTS * TERMS * (i + 1))
+            nc.sync.dma_start(
+                out=bias_w[rows, i, :],
+                in_=b_wts.unsqueeze(0).to_broadcast([PARTS, TERMS, OUTS]),
+            )
 
         rows_dram = inputs.rearrange("(p j) c -> p j c", j=SLOTS)
 
@@ -69,16 +79,16 @@ def tile_vclinear_t_e_kernel(tc, inputs, W_wts_words, W_wts_scales, b_wts, out):
 
         load_pair(0)
         load_pair(1)
-        scales_dram = W_wts_scales.bitcast(I32).rearrange("a (q r) n -> q r a n", r=4)
-        for Q in range(4):
+        scales_dram = W_wts_scales.bitcast(I32).rearrange("m (a r) n -> a r m n", r=4)
+        for a in range(4):
             nc.sync.dma_start(
-                out=scale_rows[32 * Q : 32 * Q + 4, :]
+                out=scale_rows[32 * a : 32 * a + 4, :]
                 .bitcast(I32)
-                .rearrange("r (a n) -> r a n", a=TERMS * PASSES),
-                in_=scales_dram[Q],
+                .rearrange("r (m n) -> r m n", m=TERMS * PASSES),
+                in_=scales_dram[a],
             )
         words_dram = (
-            W_wts_words.rearrange("a p n t -> a p (n t)")
+            W_wts_words.rearrange("m p n t -> m p (n t)")
             .bitcast(I32)
             .rearrange("(s g) p n -> g p s n", g=PASSES)
         )
@@ -90,7 +100,6 @@ def tile_vclinear_t_e_kernel(tc, inputs, W_wts_words, W_wts_scales, b_wts, out):
         for n in range(2, N_PAIRS):
             load_pair(n)
 
-        nc.vector.tensor_copy(out=bias_w[:], in_=bias_w_bf[:])
         nc.vector.tensor_copy(
             out=w_scales[:]
             .rearrange("p g c -> p (g c)")
@@ -99,11 +108,12 @@ def tile_vclinear_t_e_kernel(tc, inputs, W_wts_words, W_wts_scales, b_wts, out):
             in_=scale_rows[:].bitcast(I32).rearrange("p (s g n) -> p g s n", g=PASSES, s=TERMS),
         )
 
-        def spline_basis(n):
-            fn = basis[:, n, 0 : PAIR * TERMS].rearrange("p (i s) -> p i s", s=TERMS)
-            hinge = stage.tile([P, PAIR, len(KNOTS)], F32)
-            hinge_sq = stage.tile([P, PAIR, len(KNOTS)], F32)
-            nc.gpsimd.tensor_copy(out=fn[:, :, 1], in_=x_rows[:, PAIR * n : PAIR * (n + 1), T_AT])
+        for q in range(SLOTS // QUAD):
+            slots = slice(QUAD * q, QUAD * (q + 1))
+            fn = basis[:, slots, :]
+            hinge = stage.tile([P, QUAD, len(KNOTS)], F32)
+            hinge_sq = stage.tile([P, QUAD, len(KNOTS)], F32)
+            nc.gpsimd.tensor_copy(out=fn[:, :, 1], in_=x_rows[:, slots, T_AT])
             nc.gpsimd.tensor_mul(out=fn[:, :, 2], in0=fn[:, :, 1], in1=fn[:, :, 1])
             nc.gpsimd.tensor_mul(out=fn[:, :, 3], in0=fn[:, :, 2], in1=fn[:, :, 1])
             for c, knot in enumerate(KNOTS):
@@ -117,6 +127,15 @@ def tile_vclinear_t_e_kernel(tc, inputs, W_wts_words, W_wts_scales, b_wts, out):
                 )
             nc.gpsimd.tensor_mul(out=hinge_sq[:], in0=hinge[:], in1=hinge[:])
             nc.gpsimd.tensor_mul(out=fn[:, :, 4:TERMS], in0=hinge_sq[:], in1=hinge[:])
+            value = fn.rearrange("p (n i) s -> p n i s", i=PAIR)
+            part = basis_parts[
+                :, QUAD // PAIR * q : QUAD // PAIR * (q + 1), 0 : PAIR * PARTS * TERMS
+            ].rearrange("p n (i r s) -> p n i r s", i=PAIR, r=PARTS)
+            rest = stage.tile([P, QUAD // PAIR, PAIR, TERMS], F32)
+            nc.gpsimd.tensor_copy(out=part[:, :, :, 0, :], in_=value)
+            nc.gpsimd.tensor_sub(out=rest[:], in0=value, in1=part[:, :, :, 0, :])
+            nc.gpsimd.tensor_copy(out=part[:, :, :, 1, :], in_=rest[:])
+            nc.gpsimd.tensor_sub(out=part[:, :, :, 2, :], in0=rest[:], in1=part[:, :, :, 1, :])
 
         def sort_words(n):
             halves = stage.tile([P, PAIR, PASSES, HALF_WORDS, P], F32)
@@ -151,29 +170,26 @@ def tile_vclinear_t_e_kernel(tc, inputs, W_wts_words, W_wts_scales, b_wts, out):
             return x_codes, x_scales
 
         def transpose_basis(n):
-            bias_ps = psum_bias.tile([P, (1 + PAIR) * P], F32)
-            basis_t = stage.tile([P, P], F32)
-            nc.tensor.transpose(bias_ps[:, 0:P], basis[:, n, :], ident[:])
-            nc.scalar.copy(out=basis_t[:], in_=bias_ps[:, 0:P])
-            return bias_ps, basis_t
+            parts_ps = psum_small.tile([P, P], BF16, tag="small")
+            parts_t = stage.tile([P, P], BF16)
+            nc.tensor.transpose(parts_ps[:], basis_parts[:, n, :], ident_bf[:])
+            nc.scalar.copy(out=parts_t[:], in_=parts_ps[:])
+            return parts_t
 
-        def bias_term(bias_ps, basis_t):
+        def bias_term(parts_t):
+            bias_ps = psum_small.tile([P, PAIR, OUTS], F32, tag="small")
             bias_sb = stage.tile([P, PAIR, OUTS], F32)
             for i in range(PAIR):
                 nc.tensor.matmul(
-                    bias_ps[:, (1 + i) * P : (2 + i) * P],
-                    lhsT=basis_t[:],
-                    rhs=bias_w[:, i, :],
-                    start=True,
-                    stop=True,
+                    bias_ps[:, i, :], lhsT=parts_t[:], rhs=bias_w[:, i, :], start=True, stop=True
                 )
-            nc.scalar.copy(
-                out=bias_sb[:].rearrange("p i o -> p (i o)"), in_=bias_ps[:, P : (1 + PAIR) * P]
-            )
+            nc.scalar.copy(out=bias_sb[:], in_=bias_ps[:])
             return bias_sb
 
-        def multiply(x_codes, x_scales):
-            products = []
+        products = {}
+        bias_of = {}
+
+        def multiply(n, x_codes, x_scales):
             for i in range(PAIR):
                 for h in range(BANKS):
                     prod = psum_prod.tile([P, N_MOVE], F32)
@@ -189,29 +205,30 @@ def tile_vclinear_t_e_kernel(tc, inputs, W_wts_words, W_wts_scales, b_wts, out):
                             start=(g == 0),
                             stop=(g == PASSES - 1),
                         )
-                    products.append(prod)
-            return products
+                    products[(PAIR * n + i, h)] = prod
 
-        def combine(n, products, bias_sb):
-            for s in range(TERMS):
-                for i in range(PAIR):
-                    total = out_rows[:, PAIR * n + i, :]
-                    piece = products[i * BANKS + s // TERMS_PER_BANK][
-                        :, (s % TERMS_PER_BANK) * OUTS : (s % TERMS_PER_BANK + 1) * OUTS
-                    ]
-                    if s == 0:
-                        nc.vector.tensor_tensor(
-                            out=total, in0=piece, in1=bias_sb[:, i, :], op=ALU.add
-                        )
-                    else:
-                        nc.vector.scalar_tensor_tensor(
-                            out=total,
-                            in0=piece,
-                            scalar=basis[:, n, i * TERMS + s : i * TERMS + s + 1],
-                            in1=total,
-                            op0=ALU.mult,
-                            op1=ALU.add,
-                        )
+        def add_term(j, s):
+            total = out_rows[:, j, :]
+            c = s % TERMS_PER_BANK
+            piece = products[(j, s // TERMS_PER_BANK)][:, c * OUTS : (c + 1) * OUTS]
+            if s == 0:
+                nc.vector.tensor_tensor(out=total, in0=piece, in1=bias_of[j], op=ALU.add)
+            else:
+                nc.vector.scalar_tensor_tensor(
+                    out=total,
+                    in0=piece,
+                    scalar=basis[:, j, s : s + 1],
+                    in1=total,
+                    op0=ALU.mult,
+                    op1=ALU.add,
+                )
+
+        def add_terms(j):
+            for c in range(TERMS_PER_BANK):
+                if j >= 1:
+                    add_term(j - 1, TERMS_PER_BANK + c)
+                if j < SLOTS:
+                    add_term(j, c)
 
         out_dram = out.rearrange("(p j) o -> p j o", j=SLOTS)
 
@@ -219,22 +236,24 @@ def tile_vclinear_t_e_kernel(tc, inputs, W_wts_words, W_wts_scales, b_wts, out):
             slots = slice(PAIR * n, PAIR * (n + 1))
             nc.sync.dma_start(out=out_dram[:, slots, :], in_=out_rows[:, slots, :])
 
-        spline_basis(0)
         grouped_first = transpose_features(sort_words(0))
         halves_next = sort_words(1)
         quantised = quantise(grouped_first)
-        bias_tiles = transpose_basis(0)
         for n in range(N_PAIRS):
+            parts_t = transpose_basis(n)
             if n + 1 < N_PAIRS:
-                spline_basis(n + 1)
                 grouped_next = transpose_features(halves_next)
-                bias_tiles_next = transpose_basis(n + 1)
-            bias_sb = bias_term(*bias_tiles)
+            bias_sb = bias_term(parts_t)
+            for i in range(PAIR):
+                bias_of[PAIR * n + i] = bias_sb[:, i, :]
             if n + 2 < N_PAIRS:
                 halves_next = sort_words(n + 2)
-            products = multiply(*quantised)
+            multiply(n, *quantised)
             if n + 1 < N_PAIRS:
                 quantised = quantise(grouped_next)
-                bias_tiles = bias_tiles_next
-            combine(n, products, bias_sb)
-            store(n)
+            add_terms(PAIR * n)
+            if n >= 1:
+                store(n - 1)
+            add_terms(PAIR * n + 1)
+        add_terms(SLOTS)
+        store(N_PAIRS - 1)

@@ -31,6 +31,7 @@ QUAD = 4
 ROW_PITCH = 1040
 X_AT = 16
 T_AT = X_AT - 1
+SUMS = 2
 PARTS = 3
 PSUM_BANKS = 8
 PRODUCT_BANKS = PSUM_BANKS - PAIR - 1
@@ -55,6 +56,7 @@ def tile_vclinear_t_e_kernel(tc, inputs, W_wts_words, W_wts_scales, b_wts, out):
         bias_w = keep.tile([P, PAIR, OUTS], BF16)
         basis = keep.tile([P, SLOTS, TERMS], F32)
         basis_parts = keep.tile([P, N_PAIRS, P], BF16)
+        partial = keep.tile([P, SUMS, SLOTS, OUTS], F32)
         out_rows = keep.tile([P, SLOTS, OUTS], F32)
 
         make_identity(nc, ident[:])
@@ -208,11 +210,13 @@ def tile_vclinear_t_e_kernel(tc, inputs, W_wts_words, W_wts_scales, b_wts, out):
                     products[(PAIR * n + i, h)] = prod
 
         def add_term(j, s):
-            total = out_rows[:, j, :]
+            total = partial[:, s % SUMS, j, :]
             c = s % TERMS_PER_BANK
             piece = products[(j, s // TERMS_PER_BANK)][:, c * OUTS : (c + 1) * OUTS]
             if s == 0:
                 nc.vector.tensor_tensor(out=total, in0=piece, in1=bias_of[j], op=ALU.add)
+            elif s == 1:
+                nc.vector.tensor_scalar_mul(out=total, in0=piece, scalar1=basis[:, j, s : s + 1])
             else:
                 nc.vector.scalar_tensor_tensor(
                     out=total,
@@ -234,6 +238,9 @@ def tile_vclinear_t_e_kernel(tc, inputs, W_wts_words, W_wts_scales, b_wts, out):
 
         def store(n):
             slots = slice(PAIR * n, PAIR * (n + 1))
+            nc.vector.tensor_add(
+                out=out_rows[:, slots, :], in0=partial[:, 0, slots, :], in1=partial[:, 1, slots, :]
+            )
             nc.sync.dma_start(out=out_dram[:, slots, :], in_=out_rows[:, slots, :])
 
         grouped_first = transpose_features(sort_words(0))
@@ -252,8 +259,8 @@ def tile_vclinear_t_e_kernel(tc, inputs, W_wts_words, W_wts_scales, b_wts, out):
             if n + 1 < N_PAIRS:
                 quantised = quantise(grouped_next)
             add_terms(PAIR * n)
+            add_terms(PAIR * n + 1)
             if n >= 1:
                 store(n - 1)
-            add_terms(PAIR * n + 1)
         add_terms(SLOTS)
         store(N_PAIRS - 1)

@@ -27,7 +27,6 @@ TERMS_PER_BANK = TERMS // BANKS
 SLOTS = BATCH // P
 PAIR = 2
 N_PAIRS = SLOTS // PAIR
-QUAD = 4
 ROW_PITCH = 1040
 X_AT = 16
 T_AT = X_AT - 1
@@ -43,6 +42,7 @@ def tile_vclinear_t_e_kernel(tc, inputs, W_wts_words, W_wts_scales, b_wts, out):
         ctx.enter_context(tc.manual_schedule())
         keep = ctx.enter_context(tc.tile_pool(name="keep", bufs=1))
         stage = ctx.enter_context(tc.tile_pool(name="stage", bufs=3))
+        sorted_pool = ctx.enter_context(tc.tile_pool(name="sorted", bufs=3 * PAIR))
         psum_xt = ctx.enter_context(tc.psum_pool(name="psum_xt", bufs=PAIR))
         psum_prod = ctx.enter_context(tc.psum_pool(name="psum_prod", bufs=PRODUCT_BANKS))
         psum_small = ctx.enter_context(tc.psum_pool(name="psum_small", bufs=1))
@@ -110,11 +110,12 @@ def tile_vclinear_t_e_kernel(tc, inputs, W_wts_words, W_wts_scales, b_wts, out):
             in_=scale_rows[:].bitcast(I32).rearrange("p (s g n) -> p g s n", g=PASSES, s=TERMS),
         )
 
-        for q in range(SLOTS // QUAD):
-            slots = slice(QUAD * q, QUAD * (q + 1))
+        def spline_basis(first_pair, pairs):
+            count = PAIR * pairs
+            slots = slice(PAIR * first_pair, PAIR * first_pair + count)
             fn = basis[:, slots, :]
-            hinge = stage.tile([P, QUAD, len(KNOTS)], F32)
-            hinge_sq = stage.tile([P, QUAD, len(KNOTS)], F32)
+            hinge = stage.tile([P, count, len(KNOTS)], F32, tag="hinge")
+            hinge_sq = stage.tile([P, count, len(KNOTS)], F32, tag="hinge_sq")
             nc.gpsimd.tensor_copy(out=fn[:, :, 1], in_=x_rows[:, slots, T_AT])
             nc.gpsimd.tensor_mul(out=fn[:, :, 2], in0=fn[:, :, 1], in1=fn[:, :, 1])
             nc.gpsimd.tensor_mul(out=fn[:, :, 3], in0=fn[:, :, 2], in1=fn[:, :, 1])
@@ -131,31 +132,38 @@ def tile_vclinear_t_e_kernel(tc, inputs, W_wts_words, W_wts_scales, b_wts, out):
             nc.gpsimd.tensor_mul(out=fn[:, :, 4:TERMS], in0=hinge_sq[:], in1=hinge[:])
             value = fn.rearrange("p (n i) s -> p n i s", i=PAIR)
             part = basis_parts[
-                :, QUAD // PAIR * q : QUAD // PAIR * (q + 1), 0 : PAIR * PARTS * TERMS
+                :, first_pair : first_pair + pairs, 0 : PAIR * PARTS * TERMS
             ].rearrange("p n (i r s) -> p n i r s", i=PAIR, r=PARTS)
-            rest = stage.tile([P, QUAD // PAIR, PAIR, TERMS], F32)
+            rest = stage.tile([P, pairs, PAIR, TERMS], F32, tag="rest")
             nc.gpsimd.tensor_copy(out=part[:, :, :, 0, :], in_=value)
             nc.gpsimd.tensor_sub(out=rest[:], in0=value, in1=part[:, :, :, 0, :])
             nc.gpsimd.tensor_copy(out=part[:, :, :, 1, :], in_=rest[:])
             nc.gpsimd.tensor_sub(out=part[:, :, :, 2, :], in0=rest[:], in1=part[:, :, :, 1, :])
 
-        def sort_words(n):
-            halves = stage.tile([P, PAIR, PASSES, HALF_WORDS, P], F32)
-            for i in range(PAIR):
-                words = x_rows[:, PAIR * n + i, X_AT:ROW_PITCH].bitcast(F32)
-                nc.scalar.copy(
-                    out=halves[:, i],
-                    in_=words.rearrange("p (g c u) -> p g u c", g=PASSES, u=HALF_WORDS),
-                )
-            return halves
+        spline_basis(0, 1)
+        for n in range(1, N_PAIRS - 1, 2):
+            spline_basis(n, 2)
+        spline_basis(N_PAIRS - 1, 1)
 
-        def transpose_features(halves):
+        halves_of = {}
+
+        def sort_words(j):
+            halves = sorted_pool.tile([P, PASSES, HALF_WORDS, P], F32)
+            words = x_rows[:, j, X_AT:ROW_PITCH].bitcast(F32)
+            nc.scalar.copy(
+                out=halves[:], in_=words.rearrange("p (g c u) -> p g u c", g=PASSES, u=HALF_WORDS)
+            )
+            halves_of[j] = halves
+
+        def transpose_features(n):
             grouped = stage.tile([P, PAIR, PASSES, P, PACK], BF16, align_bytes=64)
             for i in range(PAIR):
                 xt = psum_xt.tile([P, PASSES, HALF_WORDS, P], F32)
                 for g in range(PASSES):
                     for u in range(HALF_WORDS):
-                        nc.tensor.transpose(xt[:, g, u, :], halves[:, i, g, u, :], ident[:])
+                        nc.tensor.transpose(
+                            xt[:, g, u, :], halves_of[PAIR * n + i][:, g, u, :], ident[:]
+                        )
                 nc.scalar.copy(
                     out=grouped[:, i].bitcast(F32), in_=xt[:].rearrange("p g u b -> p g b u")
                 )
@@ -189,50 +197,47 @@ def tile_vclinear_t_e_kernel(tc, inputs, W_wts_words, W_wts_scales, b_wts, out):
             return bias_sb
 
         products = {}
-        bias_of = {}
+        start_of = {}
 
-        def multiply(n, x_codes, x_scales):
-            for i in range(PAIR):
-                for h in range(BANKS):
-                    prod = psum_prod.tile([P, N_MOVE], F32)
-                    for g in range(PASSES):
-                        rows = slice((i * PASSES + g) * P, (i * PASSES + g + 1) * P)
-                        cols = slice(h * N_MOVE, (h + 1) * N_MOVE)
-                        nc.tensor.matmul_mx(
-                            out=prod[:],
-                            lhsT=x_codes[:, rows].bitcast(FP8X4),
-                            lhsT_scale=x_scales[:, rows],
-                            rhs=w_codes[:, g, cols].bitcast(FP8X4),
-                            rhs_scale=w_scales[:, g, cols],
-                            start=(g == 0),
-                            stop=(g == PASSES - 1),
-                        )
-                    products[(PAIR * n + i, h)] = prod
+        def multiply(j, x_codes, x_scales):
+            i = j % PAIR
+            for h in range(BANKS):
+                prod = psum_prod.tile([P, N_MOVE], F32)
+                for g in range(PASSES):
+                    rows = slice((i * PASSES + g) * P, (i * PASSES + g + 1) * P)
+                    cols = slice(h * N_MOVE, (h + 1) * N_MOVE)
+                    nc.tensor.matmul_mx(
+                        out=prod[:],
+                        lhsT=x_codes[:, rows].bitcast(FP8X4),
+                        lhsT_scale=x_scales[:, rows],
+                        rhs=w_codes[:, g, cols].bitcast(FP8X4),
+                        rhs_scale=w_scales[:, g, cols],
+                        start=(g == 0),
+                        stop=(g == PASSES - 1),
+                    )
+                products[(j, h)] = prod
+            product_0 = stage.tile([P, OUTS], F32)
+            nc.scalar.copy(out=product_0[:], in_=products[(j, 0)][:, 0:OUTS])
+            start_of[(j, 1)] = product_0[:]
 
         def add_term(j, s):
             total = partial[:, s % SUMS, j, :]
             c = s % TERMS_PER_BANK
-            piece = products[(j, s // TERMS_PER_BANK)][:, c * OUTS : (c + 1) * OUTS]
-            if s == 0:
-                nc.vector.tensor_tensor(out=total, in0=piece, in1=bias_of[j], op=ALU.add)
-            elif s == 1:
-                nc.vector.tensor_scalar_mul(out=total, in0=piece, scalar1=basis[:, j, s : s + 1])
-            else:
-                nc.vector.scalar_tensor_tensor(
-                    out=total,
-                    in0=piece,
-                    scalar=basis[:, j, s : s + 1],
-                    in1=total,
-                    op0=ALU.mult,
-                    op1=ALU.add,
-                )
+            nc.vector.scalar_tensor_tensor(
+                out=total,
+                in0=products[(j, s // TERMS_PER_BANK)][:, c * OUTS : (c + 1) * OUTS],
+                scalar=basis[:, j, s : s + 1],
+                in1=start_of.get((j, s), total),
+                op0=ALU.mult,
+                op1=ALU.add,
+            )
 
         def add_terms(j):
             for c in range(TERMS_PER_BANK):
+                if j < SLOTS and c >= 1:
+                    add_term(j, c)
                 if j >= 1:
                     add_term(j - 1, TERMS_PER_BANK + c)
-                if j < SLOTS:
-                    add_term(j, c)
 
         out_dram = out.rearrange("(p j) o -> p j o", j=SLOTS)
 
@@ -243,19 +248,22 @@ def tile_vclinear_t_e_kernel(tc, inputs, W_wts_words, W_wts_scales, b_wts, out):
             )
             nc.sync.dma_start(out=out_dram[:, slots, :], in_=out_rows[:, slots, :])
 
-        grouped_first = transpose_features(sort_words(0))
-        halves_next = sort_words(1)
+        for j in range(PAIR):
+            sort_words(j)
+        grouped_first = transpose_features(0)
+        for j in range(PAIR, 2 * PAIR):
+            sort_words(j)
         quantised = quantise(grouped_first)
         for n in range(N_PAIRS):
             parts_t = transpose_basis(n)
             if n + 1 < N_PAIRS:
-                grouped_next = transpose_features(halves_next)
+                grouped_next = transpose_features(n + 1)
             bias_sb = bias_term(parts_t)
             for i in range(PAIR):
-                bias_of[PAIR * n + i] = bias_sb[:, i, :]
-            if n + 2 < N_PAIRS:
-                halves_next = sort_words(n + 2)
-            multiply(n, *quantised)
+                start_of[(PAIR * n + i, 2)] = bias_sb[:, i, :]
+                if n + 2 < N_PAIRS:
+                    sort_words(PAIR * (n + 2) + i)
+                multiply(PAIR * n + i, *quantised)
             if n + 1 < N_PAIRS:
                 quantised = quantise(grouped_next)
             add_terms(PAIR * n)

@@ -27,6 +27,8 @@ TERMS_PER_BANK = TERMS // BANKS
 SLOTS = BATCH // P
 PAIR = 2
 N_PAIRS = SLOTS // PAIR
+QUAD = 4
+PAIRS_PER_QUAD = QUAD // PAIR
 ROW_PITCH = 1040
 X_AT = 16
 T_AT = X_AT - 1
@@ -53,25 +55,18 @@ def tile_vclinear_t_e_kernel(tc, inputs, W_wts_words, W_wts_scales, b_wts, out):
         w_codes = keep.tile([P, PASSES, TERMS * OUTS], U32, align_bytes=64)
         w_scales = keep.tile([P, PASSES, TERMS * OUTS], U8, align_bytes=64)
         scale_rows = keep.tile([P, TERMS * PASSES * OUTS], U8, align_bytes=64)
-        bias_w = keep.tile([P, PAIR, OUTS], BF16)
+        bias_w = keep.tile([P, QUAD, OUTS], BF16)
         basis = keep.tile([P, SLOTS, TERMS], F32)
-        basis_parts = keep.tile([P, N_PAIRS, P], BF16)
+        basis_parts = keep.tile([P, SLOTS // QUAD, P], BF16)
         partial = keep.tile([P, SUMS, SLOTS, OUTS], F32)
         out_rows = keep.tile([P, SLOTS, OUTS], F32)
 
         make_identity(nc, ident[:])
         make_identity(nc, ident_bf[:])
-        nc.vector.memset(bias_w[:], 0.0)
         nc.vector.memset(scale_rows[:].bitcast(I32), 0)
+        nc.vector.memset(bias_w[:], 0.0)
         nc.vector.memset(basis_parts[:], 0.0)
         nc.gpsimd.memset(basis[:, :, 0], 1.0)
-
-        for i in range(PAIR):
-            rows = slice(PARTS * TERMS * i, PARTS * TERMS * (i + 1))
-            nc.sync.dma_start(
-                out=bias_w[rows, i, :],
-                in_=b_wts.unsqueeze(0).to_broadcast([PARTS, TERMS, OUTS]),
-            )
 
         rows_dram = inputs.rearrange("(p j) c -> p j c", j=SLOTS)
 
@@ -99,6 +94,12 @@ def tile_vclinear_t_e_kernel(tc, inputs, W_wts_words, W_wts_scales, b_wts, out):
                 out=w_codes[:, g, :].bitcast(I32).rearrange("p (s n) -> p s n", s=TERMS),
                 in_=words_dram[g],
             )
+        for i in range(QUAD):
+            rows = slice(PARTS * TERMS * i, PARTS * TERMS * (i + 1))
+            nc.sync.dma_start(
+                out=bias_w[rows, i, :],
+                in_=b_wts.unsqueeze(0).to_broadcast([PARTS, TERMS, OUTS]),
+            )
         for n in range(2, N_PAIRS):
             load_pair(n)
 
@@ -110,12 +111,11 @@ def tile_vclinear_t_e_kernel(tc, inputs, W_wts_words, W_wts_scales, b_wts, out):
             in_=scale_rows[:].bitcast(I32).rearrange("p (s g n) -> p g s n", g=PASSES, s=TERMS),
         )
 
-        def spline_basis(first_pair, pairs):
-            count = PAIR * pairs
-            slots = slice(PAIR * first_pair, PAIR * first_pair + count)
+        for q in range(SLOTS // QUAD):
+            slots = slice(QUAD * q, QUAD * (q + 1))
             fn = basis[:, slots, :]
-            hinge = stage.tile([P, count, len(KNOTS)], F32, tag="hinge")
-            hinge_sq = stage.tile([P, count, len(KNOTS)], F32, tag="hinge_sq")
+            hinge = stage.tile([P, QUAD, len(KNOTS)], F32)
+            hinge_sq = stage.tile([P, QUAD, len(KNOTS)], F32)
             nc.gpsimd.tensor_copy(out=fn[:, :, 1], in_=x_rows[:, slots, T_AT])
             nc.gpsimd.tensor_mul(out=fn[:, :, 2], in0=fn[:, :, 1], in1=fn[:, :, 1])
             nc.gpsimd.tensor_mul(out=fn[:, :, 3], in0=fn[:, :, 2], in1=fn[:, :, 1])
@@ -130,22 +130,18 @@ def tile_vclinear_t_e_kernel(tc, inputs, W_wts_words, W_wts_scales, b_wts, out):
                 )
             nc.gpsimd.tensor_mul(out=hinge_sq[:], in0=hinge[:], in1=hinge[:])
             nc.gpsimd.tensor_mul(out=fn[:, :, 4:TERMS], in0=hinge_sq[:], in1=hinge[:])
-            value = fn.rearrange("p (n i) s -> p n i s", i=PAIR)
-            part = basis_parts[
-                :, first_pair : first_pair + pairs, 0 : PAIR * PARTS * TERMS
-            ].rearrange("p n (i r s) -> p n i r s", i=PAIR, r=PARTS)
-            rest = stage.tile([P, pairs, PAIR, TERMS], F32, tag="rest")
-            nc.gpsimd.tensor_copy(out=part[:, :, :, 0, :], in_=value)
-            nc.gpsimd.tensor_sub(out=rest[:], in0=value, in1=part[:, :, :, 0, :])
-            nc.gpsimd.tensor_copy(out=part[:, :, :, 1, :], in_=rest[:])
-            nc.gpsimd.tensor_sub(out=part[:, :, :, 2, :], in0=rest[:], in1=part[:, :, :, 1, :])
-
-        spline_basis(0, 1)
-        for n in range(1, N_PAIRS - 1, 2):
-            spline_basis(n, 2)
-        spline_basis(N_PAIRS - 1, 1)
+            part = basis_parts[:, q, 0 : QUAD * PARTS * TERMS].rearrange(
+                "p (i r s) -> p i r s", i=QUAD, r=PARTS
+            )
+            rest = stage.tile([P, QUAD, TERMS], F32)
+            nc.gpsimd.tensor_copy(out=part[:, :, 0, :], in_=fn)
+            nc.gpsimd.tensor_sub(out=rest[:], in0=fn, in1=part[:, :, 0, :])
+            nc.gpsimd.tensor_copy(out=part[:, :, 1, :], in_=rest[:])
+            nc.gpsimd.tensor_sub(out=part[:, :, 2, :], in0=rest[:], in1=part[:, :, 1, :])
 
         halves_of = {}
+        products = {}
+        bias_of = {}
 
         def sort_words(j):
             halves = sorted_pool.tile([P, PASSES, HALF_WORDS, P], F32)
@@ -179,25 +175,23 @@ def tile_vclinear_t_e_kernel(tc, inputs, W_wts_words, W_wts_scales, b_wts, out):
             )
             return x_codes, x_scales
 
-        def transpose_basis(n):
+        def transpose_basis(q):
             parts_ps = psum_small.tile([P, P], BF16, tag="small")
             parts_t = stage.tile([P, P], BF16)
-            nc.tensor.transpose(parts_ps[:], basis_parts[:, n, :], ident_bf[:])
+            nc.tensor.transpose(parts_ps[:], basis_parts[:, q, :], ident_bf[:])
             nc.scalar.copy(out=parts_t[:], in_=parts_ps[:])
             return parts_t
 
-        def bias_term(parts_t):
-            bias_ps = psum_small.tile([P, PAIR, OUTS], F32, tag="small")
-            bias_sb = stage.tile([P, PAIR, OUTS], F32)
-            for i in range(PAIR):
+        def bias_term(q, parts_t):
+            bias_ps = psum_small.tile([P, QUAD, OUTS], F32, tag="small")
+            bias_sb = stage.tile([P, QUAD, OUTS], F32)
+            for i in range(QUAD):
                 nc.tensor.matmul(
                     bias_ps[:, i, :], lhsT=parts_t[:], rhs=bias_w[:, i, :], start=True, stop=True
                 )
             nc.scalar.copy(out=bias_sb[:], in_=bias_ps[:])
-            return bias_sb
-
-        products = {}
-        start_of = {}
+            for i in range(QUAD):
+                bias_of[QUAD * q + i] = bias_sb[:, i, :]
 
         def multiply(j, x_codes, x_scales):
             i = j % PAIR
@@ -216,25 +210,27 @@ def tile_vclinear_t_e_kernel(tc, inputs, W_wts_words, W_wts_scales, b_wts, out):
                         stop=(g == PASSES - 1),
                     )
                 products[(j, h)] = prod
-            product_0 = stage.tile([P, OUTS], F32)
-            nc.scalar.copy(out=product_0[:], in_=products[(j, 0)][:, 0:OUTS])
-            start_of[(j, 1)] = product_0[:]
 
         def add_term(j, s):
             total = partial[:, s % SUMS, j, :]
             c = s % TERMS_PER_BANK
-            nc.vector.scalar_tensor_tensor(
-                out=total,
-                in0=products[(j, s // TERMS_PER_BANK)][:, c * OUTS : (c + 1) * OUTS],
-                scalar=basis[:, j, s : s + 1],
-                in1=start_of.get((j, s), total),
-                op0=ALU.mult,
-                op1=ALU.add,
-            )
+            piece = products[(j, s // TERMS_PER_BANK)][:, c * OUTS : (c + 1) * OUTS]
+            weight = basis[:, j, s : s + 1]
+            if s == 1:
+                nc.vector.tensor_scalar_mul(out=total, in0=piece, scalar1=weight)
+            else:
+                nc.vector.scalar_tensor_tensor(
+                    out=total,
+                    in0=piece,
+                    scalar=weight,
+                    in1=bias_of[j] if s == 0 else total,
+                    op0=ALU.mult,
+                    op1=ALU.add,
+                )
 
         def add_terms(j):
             for c in range(TERMS_PER_BANK):
-                if j < SLOTS and c >= 1:
+                if j < SLOTS:
                     add_term(j, c)
                 if j >= 1:
                     add_term(j - 1, TERMS_PER_BANK + c)
@@ -243,7 +239,7 @@ def tile_vclinear_t_e_kernel(tc, inputs, W_wts_words, W_wts_scales, b_wts, out):
 
         def store(n):
             slots = slice(PAIR * n, PAIR * (n + 1))
-            nc.vector.tensor_add(
+            nc.gpsimd.tensor_add(
                 out=out_rows[:, slots, :], in0=partial[:, 0, slots, :], in1=partial[:, 1, slots, :]
             )
             nc.sync.dma_start(out=out_dram[:, slots, :], in_=out_rows[:, slots, :])
@@ -255,12 +251,14 @@ def tile_vclinear_t_e_kernel(tc, inputs, W_wts_words, W_wts_scales, b_wts, out):
             sort_words(j)
         quantised = quantise(grouped_first)
         for n in range(N_PAIRS):
-            parts_t = transpose_basis(n)
+            opens_quad = n % PAIRS_PER_QUAD == 0
+            if opens_quad:
+                parts_t = transpose_basis(n // PAIRS_PER_QUAD)
             if n + 1 < N_PAIRS:
                 grouped_next = transpose_features(n + 1)
-            bias_sb = bias_term(parts_t)
+            if opens_quad:
+                bias_term(n // PAIRS_PER_QUAD, parts_t)
             for i in range(PAIR):
-                start_of[(PAIR * n + i, 2)] = bias_sb[:, i, :]
                 if n + 2 < N_PAIRS:
                     sort_words(PAIR * (n + 2) + i)
                 multiply(PAIR * n + i, *quantised)

@@ -66,7 +66,6 @@ def tile_vclinear_t_e_kernel(tc, inputs, W_wts_words, W_wts_scales, b_wts, out):
         nc.vector.memset(scale_rows[:].bitcast(I32), 0)
         nc.vector.memset(bias_w[:], 0.0)
         nc.vector.memset(basis_parts[:], 0.0)
-        nc.gpsimd.memset(basis[:, :, 0], 1.0)
 
         rows_dram = inputs.rearrange("(p j) c -> p j c", j=SLOTS)
 
@@ -103,24 +102,17 @@ def tile_vclinear_t_e_kernel(tc, inputs, W_wts_words, W_wts_scales, b_wts, out):
         for n in range(2, N_PAIRS):
             load_pair(n)
 
-        nc.vector.tensor_copy(
-            out=w_scales[:]
-            .rearrange("p g c -> p (g c)")
-            .bitcast(I32)
-            .rearrange("p (g s n) -> p g s n", g=PASSES, s=TERMS),
-            in_=scale_rows[:].bitcast(I32).rearrange("p (s g n) -> p g s n", g=PASSES, s=TERMS),
-        )
-
-        for q in range(SLOTS // QUAD):
+        def spline_basis(engine, q):
             slots = slice(QUAD * q, QUAD * (q + 1))
             fn = basis[:, slots, :]
             hinge = stage.tile([P, QUAD, len(KNOTS)], F32)
             hinge_sq = stage.tile([P, QUAD, len(KNOTS)], F32)
-            nc.gpsimd.tensor_copy(out=fn[:, :, 1], in_=x_rows[:, slots, T_AT])
-            nc.gpsimd.tensor_mul(out=fn[:, :, 2], in0=fn[:, :, 1], in1=fn[:, :, 1])
-            nc.gpsimd.tensor_mul(out=fn[:, :, 3], in0=fn[:, :, 2], in1=fn[:, :, 1])
+            engine.memset(fn[:, :, 0], 1.0)
+            engine.tensor_copy(out=fn[:, :, 1], in_=x_rows[:, slots, T_AT])
+            engine.tensor_mul(out=fn[:, :, 2], in0=fn[:, :, 1], in1=fn[:, :, 1])
+            engine.tensor_mul(out=fn[:, :, 3], in0=fn[:, :, 2], in1=fn[:, :, 1])
             for c, knot in enumerate(KNOTS):
-                nc.gpsimd.tensor_scalar(
+                engine.tensor_scalar(
                     out=hinge[:, :, c],
                     in0=fn[:, :, 1],
                     scalar1=knot,
@@ -128,16 +120,28 @@ def tile_vclinear_t_e_kernel(tc, inputs, W_wts_words, W_wts_scales, b_wts, out):
                     op0=ALU.subtract,
                     op1=ALU.max,
                 )
-            nc.gpsimd.tensor_mul(out=hinge_sq[:], in0=hinge[:], in1=hinge[:])
-            nc.gpsimd.tensor_mul(out=fn[:, :, 4:TERMS], in0=hinge_sq[:], in1=hinge[:])
+            engine.tensor_mul(out=hinge_sq[:], in0=hinge[:], in1=hinge[:])
+            engine.tensor_mul(out=fn[:, :, 4:TERMS], in0=hinge_sq[:], in1=hinge[:])
             part = basis_parts[:, q, 0 : QUAD * PARTS * TERMS].rearrange(
                 "p (i r s) -> p i r s", i=QUAD, r=PARTS
             )
             rest = stage.tile([P, QUAD, TERMS], F32)
-            nc.gpsimd.tensor_copy(out=part[:, :, 0, :], in_=fn)
-            nc.gpsimd.tensor_sub(out=rest[:], in0=fn, in1=part[:, :, 0, :])
-            nc.gpsimd.tensor_copy(out=part[:, :, 1, :], in_=rest[:])
-            nc.gpsimd.tensor_sub(out=part[:, :, 2, :], in0=rest[:], in1=part[:, :, 1, :])
+            engine.tensor_copy(out=part[:, :, 0, :], in_=fn)
+            engine.tensor_sub(out=rest[:], in0=fn, in1=part[:, :, 0, :])
+            engine.tensor_copy(out=part[:, :, 1, :], in_=rest[:])
+            engine.tensor_sub(out=part[:, :, 2, :], in0=rest[:], in1=part[:, :, 1, :])
+
+        spline_basis(nc.vector, 0)
+        for q in range(1, SLOTS // QUAD):
+            spline_basis(nc.gpsimd, q)
+
+        nc.vector.tensor_copy(
+            out=w_scales[:]
+            .rearrange("p g c -> p (g c)")
+            .bitcast(I32)
+            .rearrange("p (g s n) -> p g s n", g=PASSES, s=TERMS),
+            in_=scale_rows[:].bitcast(I32).rearrange("p (s g n) -> p g s n", g=PASSES, s=TERMS),
+        )
 
         halves_of = {}
         products = {}

@@ -31,7 +31,7 @@ QUAD = 4
 PAIRS_PER_QUAD = QUAD // PAIR
 ROW_PITCH = 1040
 X_AT = 16
-T_AT = X_AT - 1
+T_PIECE = 2
 SUMS = 2
 PARTS = 3
 PSUM_BANKS = 8
@@ -52,6 +52,7 @@ def tile_vclinear_t_e_kernel(tc, inputs, W_wts_words, W_wts_scales, b_wts, out):
         ident = keep.tile([P, P], F32)
         ident_bf = keep.tile([P, P], BF16)
         x_rows = keep.tile([P, SLOTS, ROW_PITCH], BF16, align_bytes=64)
+        t_rows = keep.tile([P, SLOTS, T_PIECE], BF16)
         w_codes = keep.tile([P, PASSES, TERMS * OUTS], U32, align_bytes=64)
         w_scales = keep.tile([P, PASSES, TERMS * OUTS], U8, align_bytes=64)
         scale_rows = keep.tile([P, TERMS * PASSES * OUTS], U8, align_bytes=64)
@@ -71,8 +72,14 @@ def tile_vclinear_t_e_kernel(tc, inputs, W_wts_words, W_wts_scales, b_wts, out):
 
         def load_pair(n):
             slots = slice(PAIR * n, PAIR * (n + 1))
-            nc.sync.dma_start(out=x_rows[:, slots, T_AT:ROW_PITCH], in_=rows_dram[:, slots, :])
+            nc.sync.dma_start(out=x_rows[:, slots, X_AT:ROW_PITCH], in_=rows_dram[:, slots, 1:])
 
+        def load_treatments(first, last):
+            nc.sync.dma_start(
+                out=t_rows[:, first:last, :], in_=rows_dram[:, first:last, 0:T_PIECE]
+            )
+
+        load_treatments(0, QUAD)
         load_pair(0)
         load_pair(1)
         scales_dram = W_wts_scales.bitcast(I32).rearrange("m (a r) n -> a r m n", r=4)
@@ -99,6 +106,7 @@ def tile_vclinear_t_e_kernel(tc, inputs, W_wts_words, W_wts_scales, b_wts, out):
                 out=bias_w[rows, i, :],
                 in_=b_wts.unsqueeze(0).to_broadcast([PARTS, TERMS, OUTS]),
             )
+        load_treatments(QUAD, SLOTS)
         for n in range(2, N_PAIRS):
             load_pair(n)
 
@@ -108,7 +116,7 @@ def tile_vclinear_t_e_kernel(tc, inputs, W_wts_words, W_wts_scales, b_wts, out):
             hinge = stage.tile([P, QUAD, len(KNOTS)], F32)
             hinge_sq = stage.tile([P, QUAD, len(KNOTS)], F32)
             engine.memset(fn[:, :, 0], 1.0)
-            engine.tensor_copy(out=fn[:, :, 1], in_=x_rows[:, slots, T_AT])
+            engine.tensor_copy(out=fn[:, :, 1], in_=t_rows[:, slots, 0])
             engine.tensor_mul(out=fn[:, :, 2], in0=fn[:, :, 1], in1=fn[:, :, 1])
             engine.tensor_mul(out=fn[:, :, 3], in0=fn[:, :, 2], in1=fn[:, :, 1])
             for c, knot in enumerate(KNOTS):

@@ -10,6 +10,7 @@ U32 = mybir.dt.uint32
 U8 = mybir.dt.uint8
 FP8X4 = mybir.dt.float8_e4m3fn_x4
 ALU = mybir.AluOpType
+ACT = mybir.ActivationFunctionType
 
 P = 128
 BATCH, FEATURES, OUTS, TERMS = 4096, 1024, 128, 8
@@ -20,22 +21,23 @@ PACK = 4
 K_PASS = P * PACK
 PASSES = FEATURES // K_PASS
 HALF_WORDS = 2
-N_MOVE = 512
-BANKS = TERMS * OUTS // N_MOVE
-TERMS_PER_BANK = TERMS // BANKS
 
 SLOTS = BATCH // P
 PAIR = 2
 N_PAIRS = SLOTS // PAIR
 QUAD = 4
-PAIRS_PER_QUAD = QUAD // PAIR
-ROW_PITCH = 1040
-X_AT = 16
+N_QUADS = SLOTS // QUAD
+BANK_TERMS = 2
+N_MOVE = BANK_TERMS * OUTS
+BANKS = TERMS // BANK_TERMS
+BANK_COLS = PAIR * N_MOVE
 T_PIECE = 2
 SUMS = 2
 PARTS = 3
+HEAD_SLOTS = 2 * QUAD
 PSUM_BANKS = 8
 PRODUCT_BANKS = PSUM_BANKS - PAIR - 1
+FIRST_SHARED_SORT = 5
 
 
 def tile_vclinear_t_e_kernel(tc, inputs, W_wts_words, W_wts_scales, b_wts, out):
@@ -44,21 +46,23 @@ def tile_vclinear_t_e_kernel(tc, inputs, W_wts_words, W_wts_scales, b_wts, out):
         ctx.enter_context(tc.manual_schedule())
         keep = ctx.enter_context(tc.tile_pool(name="keep", bufs=1))
         stage = ctx.enter_context(tc.tile_pool(name="stage", bufs=3))
-        sorted_pool = ctx.enter_context(tc.tile_pool(name="sorted", bufs=3 * PAIR))
+        sorted_pool = ctx.enter_context(tc.tile_pool(name="sorted", bufs=4 * PAIR))
         psum_xt = ctx.enter_context(tc.psum_pool(name="psum_xt", bufs=PAIR))
         psum_prod = ctx.enter_context(tc.psum_pool(name="psum_prod", bufs=PRODUCT_BANKS))
         psum_small = ctx.enter_context(tc.psum_pool(name="psum_small", bufs=1))
 
         ident = keep.tile([P, P], F32)
         ident_bf = keep.tile([P, P], BF16)
-        x_rows = keep.tile([P, SLOTS, ROW_PITCH], BF16, align_bytes=64)
+        x_rows = keep.tile([P, SLOTS, FEATURES], BF16, align_bytes=64)
         t_rows = keep.tile([P, SLOTS, T_PIECE], BF16)
         w_codes = keep.tile([P, PASSES, TERMS * OUTS], U32, align_bytes=64)
         w_scales = keep.tile([P, PASSES, TERMS * OUTS], U8, align_bytes=64)
         scale_rows = keep.tile([P, TERMS * PASSES * OUTS], U8, align_bytes=64)
         bias_w = keep.tile([P, QUAD, OUTS], BF16)
         basis = keep.tile([P, SLOTS, TERMS], F32)
-        basis_parts = keep.tile([P, SLOTS // QUAD, P], BF16)
+        basis_parts = keep.tile([P, N_QUADS, P], BF16)
+        first_product = keep.tile([P, SLOTS, OUTS], F32)
+        second_term = keep.tile([P, SLOTS, OUTS], F32)
         partial = keep.tile([P, SUMS, SLOTS, OUTS], F32)
         out_rows = keep.tile([P, SLOTS, OUTS], F32)
 
@@ -72,14 +76,15 @@ def tile_vclinear_t_e_kernel(tc, inputs, W_wts_words, W_wts_scales, b_wts, out):
 
         def load_pair(n):
             slots = slice(PAIR * n, PAIR * (n + 1))
-            nc.sync.dma_start(out=x_rows[:, slots, X_AT:ROW_PITCH], in_=rows_dram[:, slots, 1:])
+            nc.sync.dma_start(out=x_rows[:, slots, :], in_=rows_dram[:, slots, 1:])
 
         def load_treatments(first, last):
-            nc.sync.dma_start(
+            nc.scalar.dma_start(
                 out=t_rows[:, first:last, :], in_=rows_dram[:, first:last, 0:T_PIECE]
             )
 
-        load_treatments(0, QUAD)
+        load_treatments(0, HEAD_SLOTS)
+        load_treatments(HEAD_SLOTS, SLOTS)
         load_pair(0)
         load_pair(1)
         scales_dram = W_wts_scales.bitcast(I32).rearrange("m (a r) n -> a r m n", r=4)
@@ -106,15 +111,16 @@ def tile_vclinear_t_e_kernel(tc, inputs, W_wts_words, W_wts_scales, b_wts, out):
                 out=bias_w[rows, i, :],
                 in_=b_wts.unsqueeze(0).to_broadcast([PARTS, TERMS, OUTS]),
             )
-        load_treatments(QUAD, SLOTS)
         for n in range(2, N_PAIRS):
             load_pair(n)
 
-        def spline_basis(engine, q):
-            slots = slice(QUAD * q, QUAD * (q + 1))
+        def spline_basis(engine, first, last):
+            count = last - first
+            slots = slice(first, last)
             fn = basis[:, slots, :]
-            hinge = stage.tile([P, QUAD, len(KNOTS)], F32)
-            hinge_sq = stage.tile([P, QUAD, len(KNOTS)], F32)
+            hinge = keep.tile([P, count, len(KNOTS)], F32, name="hinge_%d" % first)
+            hinge_sq = keep.tile([P, count, len(KNOTS)], F32, name="hinge_sq_%d" % first)
+            rest = keep.tile([P, count, TERMS], F32, name="rest_%d" % first)
             engine.memset(fn[:, :, 0], 1.0)
             engine.tensor_copy(out=fn[:, :, 1], in_=t_rows[:, slots, 0])
             engine.tensor_mul(out=fn[:, :, 2], in0=fn[:, :, 1], in1=fn[:, :, 1])
@@ -130,18 +136,18 @@ def tile_vclinear_t_e_kernel(tc, inputs, W_wts_words, W_wts_scales, b_wts, out):
                 )
             engine.tensor_mul(out=hinge_sq[:], in0=hinge[:], in1=hinge[:])
             engine.tensor_mul(out=fn[:, :, 4:TERMS], in0=hinge_sq[:], in1=hinge[:])
-            part = basis_parts[:, q, 0 : QUAD * PARTS * TERMS].rearrange(
-                "p (i r s) -> p i r s", i=QUAD, r=PARTS
+            part = basis_parts[:, first // QUAD : last // QUAD, 0 : QUAD * PARTS * TERMS].rearrange(
+                "p q (i r s) -> p q i r s", i=QUAD, r=PARTS
             )
-            rest = stage.tile([P, QUAD, TERMS], F32)
-            engine.tensor_copy(out=part[:, :, 0, :], in_=fn)
-            engine.tensor_sub(out=rest[:], in0=fn, in1=part[:, :, 0, :])
-            engine.tensor_copy(out=part[:, :, 1, :], in_=rest[:])
-            engine.tensor_sub(out=part[:, :, 2, :], in0=rest[:], in1=part[:, :, 1, :])
+            fn_q = fn.rearrange("p (q i) s -> p q i s", i=QUAD)
+            rest_q = rest[:].rearrange("p (q i) s -> p q i s", i=QUAD)
+            engine.tensor_copy(out=part[:, :, :, 0, :], in_=fn_q)
+            engine.tensor_sub(out=rest_q, in0=fn_q, in1=part[:, :, :, 0, :])
+            engine.tensor_copy(out=part[:, :, :, 1, :], in_=rest_q)
+            engine.tensor_sub(out=part[:, :, :, 2, :], in0=rest_q, in1=part[:, :, :, 1, :])
 
-        spline_basis(nc.vector, 0)
-        for q in range(1, SLOTS // QUAD):
-            spline_basis(nc.gpsimd, q)
+        spline_basis(nc.vector, 0, HEAD_SLOTS)
+        spline_basis(nc.gpsimd, HEAD_SLOTS, SLOTS)
 
         nc.vector.tensor_copy(
             out=w_scales[:]
@@ -152,16 +158,23 @@ def tile_vclinear_t_e_kernel(tc, inputs, W_wts_words, W_wts_scales, b_wts, out):
         )
 
         halves_of = {}
+        grouped_of = {}
         products = {}
         bias_of = {}
 
-        def sort_words(j):
+        def sort_words(j, on_gpsimd):
             halves = sorted_pool.tile([P, PASSES, HALF_WORDS, P], F32)
-            words = x_rows[:, j, X_AT:ROW_PITCH].bitcast(F32)
-            nc.scalar.copy(
-                out=halves[:], in_=words.rearrange("p (g c u) -> p g u c", g=PASSES, u=HALF_WORDS)
-            )
+            words = x_rows[:, j, :].bitcast(F32)
+            source = words.rearrange("p (g c u) -> p g u c", g=PASSES, u=HALF_WORDS)
+            if on_gpsimd:
+                nc.gpsimd.tensor_copy(out=halves[:], in_=source)
+            else:
+                nc.scalar.copy(out=halves[:], in_=source)
             halves_of[j] = halves
+
+        def sort_pair(n):
+            sort_words(PAIR * n, False)
+            sort_words(PAIR * n + 1, n >= FIRST_SHARED_SORT)
 
         def transpose_features(n):
             grouped = stage.tile([P, PAIR, PASSES, P, PACK], BF16, align_bytes=64)
@@ -175,15 +188,15 @@ def tile_vclinear_t_e_kernel(tc, inputs, W_wts_words, W_wts_scales, b_wts, out):
                 nc.scalar.copy(
                     out=grouped[:, i].bitcast(F32), in_=xt[:].rearrange("p g u b -> p g b u")
                 )
-            return grouped
+            grouped_of[n] = grouped
 
-        def quantise(grouped):
+        def quantise(n):
             x_codes = stage.tile([P, PAIR * PASSES * P], U32, align_bytes=64)
             x_scales = stage.tile([P, PAIR * PASSES * P], U8, align_bytes=64)
             nc.vector.quantize_mx(
                 out=x_codes[:].bitcast(FP8X4),
                 scales=x_scales[:],
-                in_=grouped[:].rearrange("p i g b t -> p (i g b t)"),
+                in_=grouped_of[n][:].rearrange("p i g b t -> p (i g b t)"),
             )
             return x_codes, x_scales
 
@@ -197,88 +210,108 @@ def tile_vclinear_t_e_kernel(tc, inputs, W_wts_words, W_wts_scales, b_wts, out):
         def bias_term(q, parts_t):
             bias_ps = psum_small.tile([P, QUAD, OUTS], F32, tag="small")
             bias_sb = stage.tile([P, QUAD, OUTS], F32)
-            for i in range(QUAD):
-                nc.tensor.matmul(
-                    bias_ps[:, i, :], lhsT=parts_t[:], rhs=bias_w[:, i, :], start=True, stop=True
-                )
+            nc.tensor.matmul(
+                bias_ps[:].rearrange("p i o -> p (i o)"),
+                lhsT=parts_t[:],
+                rhs=bias_w[:].rearrange("p i o -> p (i o)"),
+                start=True,
+                stop=True,
+            )
             nc.scalar.copy(out=bias_sb[:], in_=bias_ps[:])
             for i in range(QUAD):
                 bias_of[QUAD * q + i] = bias_sb[:, i, :]
 
-        def multiply(j, x_codes, x_scales):
-            i = j % PAIR
+        def multiply(n, x_codes, x_scales):
             for h in range(BANKS):
-                prod = psum_prod.tile([P, N_MOVE], F32)
-                for g in range(PASSES):
-                    rows = slice((i * PASSES + g) * P, (i * PASSES + g + 1) * P)
-                    cols = slice(h * N_MOVE, (h + 1) * N_MOVE)
-                    nc.tensor.matmul_mx(
-                        out=prod[:],
-                        lhsT=x_codes[:, rows].bitcast(FP8X4),
-                        lhsT_scale=x_scales[:, rows],
-                        rhs=w_codes[:, g, cols].bitcast(FP8X4),
-                        rhs_scale=w_scales[:, g, cols],
-                        start=(g == 0),
-                        stop=(g == PASSES - 1),
-                    )
-                products[(j, h)] = prod
+                prod = psum_prod.tile([P, PAIR, BANK_TERMS, OUTS], F32)
+                cols = slice(h * N_MOVE, (h + 1) * N_MOVE)
+                for i in range(PAIR):
+                    for g in range(PASSES):
+                        rows = slice((i * PASSES + g) * P, (i * PASSES + g + 1) * P)
+                        nc.tensor.matmul_mx(
+                            out=prod[:, i].rearrange("p s o -> p (s o)"),
+                            lhsT=x_codes[:, rows].bitcast(FP8X4),
+                            lhsT_scale=x_scales[:, rows],
+                            rhs=w_codes[:, g, cols].bitcast(FP8X4),
+                            rhs_scale=w_scales[:, g, cols],
+                            start=(g == 0),
+                            stop=(g == PASSES - 1),
+                        )
+                products[(n, h)] = prod
 
-        def add_term(j, s):
-            total = partial[:, s % SUMS, j, :]
-            c = s % TERMS_PER_BANK
-            piece = products[(j, s // TERMS_PER_BANK)][:, c * OUTS : (c + 1) * OUTS]
-            weight = basis[:, j, s : s + 1]
-            if s == 1:
-                nc.vector.tensor_scalar_mul(out=total, in0=piece, scalar1=weight)
-            else:
-                nc.vector.scalar_tensor_tensor(
-                    out=total,
-                    in0=piece,
-                    scalar=weight,
-                    in1=bias_of[j] if s == 0 else total,
-                    op0=ALU.mult,
-                    op1=ALU.add,
+        def scalar_terms(n):
+            slots = slice(PAIR * n, PAIR * (n + 1))
+            prod = products[(n, 0)]
+            nc.scalar.copy(out=first_product[:, slots, :], in_=prod[:, :, 0, :])
+            for i in range(PAIR):
+                j = PAIR * n + i
+                nc.scalar.activation(
+                    out=second_term[:, j, :],
+                    in_=prod[:, i, 1, :],
+                    func=ACT.Copy,
+                    scale=basis[:, j, 1:2],
                 )
 
-        def add_terms(j):
-            for c in range(TERMS_PER_BANK):
-                if j < SLOTS:
-                    add_term(j, c)
-                if j >= 1:
-                    add_term(j - 1, TERMS_PER_BANK + c)
+        def add_terms(n, h):
+            for i in range(PAIR):
+                j = PAIR * n + i
+                for c in range(BANK_TERMS):
+                    total = partial[:, c, j, :]
+                    if h > 1:
+                        before = total
+                    elif c == 0:
+                        before = bias_of[j]
+                    else:
+                        before = first_product[:, j, :]
+                    s = BANK_TERMS * h + c
+                    nc.vector.scalar_tensor_tensor(
+                        out=total,
+                        in0=products[(n, h)][:, i, c, :],
+                        scalar=basis[:, j, s : s + 1],
+                        in1=before,
+                        op0=ALU.mult,
+                        op1=ALU.add,
+                    )
 
         out_dram = out.rearrange("(p j) o -> p j o", j=SLOTS)
 
         def store(n):
             slots = slice(PAIR * n, PAIR * (n + 1))
+            both = stage.tile([P, PAIR, OUTS], F32)
             nc.gpsimd.tensor_add(
-                out=out_rows[:, slots, :], in0=partial[:, 0, slots, :], in1=partial[:, 1, slots, :]
+                out=both[:], in0=partial[:, 0, slots, :], in1=partial[:, 1, slots, :]
+            )
+            nc.gpsimd.tensor_add(
+                out=out_rows[:, slots, :], in0=both[:], in1=second_term[:, slots, :]
             )
             nc.sync.dma_start(out=out_dram[:, slots, :], in_=out_rows[:, slots, :])
 
-        for j in range(PAIR):
-            sort_words(j)
-        grouped_first = transpose_features(0)
-        for j in range(PAIR, 2 * PAIR):
-            sort_words(j)
-        quantised = quantise(grouped_first)
+        sort_pair(0)
+        transpose_features(0)
+        parts_t = transpose_basis(0)
+        sort_pair(1)
+        transpose_features(1)
+        bias_term(0, parts_t)
+        quantised = quantise(0)
         for n in range(N_PAIRS):
-            opens_quad = n % PAIRS_PER_QUAD == 0
-            if opens_quad:
-                parts_t = transpose_basis(n // PAIRS_PER_QUAD)
+            multiply(n, *quantised)
+            scalar_terms(n)
+            if n == 0:
+                sort_pair(2)
             if n + 1 < N_PAIRS:
-                grouped_next = transpose_features(n + 1)
+                quantised = quantise(n + 1)
+            next_quad = (n + 1) // PAIR
+            opens_quad = n % PAIR == 1 and next_quad < N_QUADS
             if opens_quad:
-                bias_term(n // PAIRS_PER_QUAD, parts_t)
-            for i in range(PAIR):
-                if n + 2 < N_PAIRS:
-                    sort_words(PAIR * (n + 2) + i)
-                multiply(PAIR * n + i, *quantised)
-            if n + 1 < N_PAIRS:
-                quantised = quantise(grouped_next)
-            add_terms(PAIR * n)
-            add_terms(PAIR * n + 1)
+                parts_t = transpose_basis(next_quad)
+            if n + 2 < N_PAIRS:
+                transpose_features(n + 2)
+            if opens_quad:
+                bias_term(next_quad, parts_t)
+            if n + 3 < N_PAIRS:
+                sort_pair(n + 3)
+            for h in range(1, BANKS):
+                add_terms(n, h)
             if n >= 1:
                 store(n - 1)
-        add_terms(SLOTS)
         store(N_PAIRS - 1)

@@ -36,7 +36,7 @@ SUMS = 2
 PARTS = 3
 HEAD_SLOTS = 2 * QUAD
 PSUM_BANKS = 8
-PRODUCT_BANKS = PSUM_BANKS - PAIR - 1
+ROTATING_BANKS = PSUM_BANKS - 1
 FIRST_SHARED_SORT = 5
 
 
@@ -47,8 +47,7 @@ def tile_vclinear_t_e_kernel(tc, inputs, W_wts_words, W_wts_scales, b_wts, out):
         keep = ctx.enter_context(tc.tile_pool(name="keep", bufs=1))
         stage = ctx.enter_context(tc.tile_pool(name="stage", bufs=3))
         sorted_pool = ctx.enter_context(tc.tile_pool(name="sorted", bufs=4 * PAIR))
-        psum_xt = ctx.enter_context(tc.psum_pool(name="psum_xt", bufs=PAIR))
-        psum_prod = ctx.enter_context(tc.psum_pool(name="psum_prod", bufs=PRODUCT_BANKS))
+        psum = ctx.enter_context(tc.psum_pool(name="psum", bufs=ROTATING_BANKS))
         psum_small = ctx.enter_context(tc.psum_pool(name="psum_small", bufs=1))
 
         ident = keep.tile([P, P], F32)
@@ -79,12 +78,11 @@ def tile_vclinear_t_e_kernel(tc, inputs, W_wts_words, W_wts_scales, b_wts, out):
             nc.sync.dma_start(out=x_rows[:, slots, :], in_=rows_dram[:, slots, 1:])
 
         def load_treatments(first, last):
-            nc.scalar.dma_start(
+            nc.sync.dma_start(
                 out=t_rows[:, first:last, :], in_=rows_dram[:, first:last, 0:T_PIECE]
             )
 
         load_treatments(0, HEAD_SLOTS)
-        load_treatments(HEAD_SLOTS, SLOTS)
         load_pair(0)
         load_pair(1)
         scales_dram = W_wts_scales.bitcast(I32).rearrange("m (a r) n -> a r m n", r=4)
@@ -107,10 +105,11 @@ def tile_vclinear_t_e_kernel(tc, inputs, W_wts_words, W_wts_scales, b_wts, out):
             )
         for i in range(QUAD):
             rows = slice(PARTS * TERMS * i, PARTS * TERMS * (i + 1))
-            nc.sync.dma_start(
+            nc.scalar.dma_start(
                 out=bias_w[rows, i, :],
                 in_=b_wts.unsqueeze(0).to_broadcast([PARTS, TERMS, OUTS]),
             )
+        load_treatments(HEAD_SLOTS, SLOTS)
         for n in range(2, N_PAIRS):
             load_pair(n)
 
@@ -147,18 +146,21 @@ def tile_vclinear_t_e_kernel(tc, inputs, W_wts_words, W_wts_scales, b_wts, out):
             engine.tensor_sub(out=part[:, :, :, 2, :], in0=rest_q, in1=part[:, :, :, 1, :])
 
         spline_basis(nc.vector, 0, HEAD_SLOTS)
-        spline_basis(nc.gpsimd, HEAD_SLOTS, SLOTS)
 
-        nc.vector.tensor_copy(
+        nc.gpsimd.tensor_copy(
             out=w_scales[:]
             .rearrange("p g c -> p (g c)")
             .bitcast(I32)
             .rearrange("p (g s n) -> p g s n", g=PASSES, s=TERMS),
             in_=scale_rows[:].bitcast(I32).rearrange("p (s g n) -> p g s n", g=PASSES, s=TERMS),
         )
+        spline_basis(nc.gpsimd, HEAD_SLOTS, SLOTS)
 
         halves_of = {}
+        xt_of = {}
         grouped_of = {}
+        quantised_of = {}
+        bias_ps_of = {}
         products = {}
         bias_of = {}
 
@@ -176,19 +178,28 @@ def tile_vclinear_t_e_kernel(tc, inputs, W_wts_words, W_wts_scales, b_wts, out):
             sort_words(PAIR * n, False)
             sort_words(PAIR * n + 1, n >= FIRST_SHARED_SORT)
 
-        def transpose_features(n):
-            grouped = stage.tile([P, PAIR, PASSES, P, PACK], BF16, align_bytes=64)
-            for i in range(PAIR):
-                xt = psum_xt.tile([P, PASSES, HALF_WORDS, P], F32)
-                for g in range(PASSES):
-                    for u in range(HALF_WORDS):
-                        nc.tensor.transpose(
-                            xt[:, g, u, :], halves_of[PAIR * n + i][:, g, u, :], ident[:]
-                        )
-                nc.scalar.copy(
-                    out=grouped[:, i].bitcast(F32), in_=xt[:].rearrange("p g u b -> p g b u")
-                )
-            grouped_of[n] = grouped
+        def transpose_slot(j):
+            xt = psum.tile([P, PASSES, HALF_WORDS, P], F32, tag="bank")
+            words = x_rows[:, j, :].bitcast(F32)
+            for g in range(PASSES):
+                for u in range(HALF_WORDS):
+                    if j in halves_of:
+                        source = halves_of[j][:, g, u, :]
+                    else:
+                        first_word = g * HALF_WORDS * P + u
+                        source = words[:, first_word : (g + 1) * HALF_WORDS * P : HALF_WORDS]
+                    nc.tensor.transpose(xt[:, g, u, :], source, ident[:])
+            xt_of[j] = xt
+
+        def group_slot(j):
+            n, i = divmod(j, PAIR)
+            if i == 0:
+                grouped = stage.tile([P, PAIR, PASSES, P, PACK], BF16, align_bytes=64)
+                grouped_of[n] = grouped
+            nc.scalar.copy(
+                out=grouped_of[n][:, i].bitcast(F32),
+                in_=xt_of[j][:].rearrange("p g u b -> p g b u"),
+            )
 
         def quantise(n):
             x_codes = stage.tile([P, PAIR * PASSES * P], U32, align_bytes=64)
@@ -198,7 +209,7 @@ def tile_vclinear_t_e_kernel(tc, inputs, W_wts_words, W_wts_scales, b_wts, out):
                 scales=x_scales[:],
                 in_=grouped_of[n][:].rearrange("p i g b t -> p (i g b t)"),
             )
-            return x_codes, x_scales
+            quantised_of[n] = (x_codes, x_scales)
 
         def transpose_basis(q):
             parts_ps = psum_small.tile([P, P], BF16, tag="small")
@@ -207,9 +218,8 @@ def tile_vclinear_t_e_kernel(tc, inputs, W_wts_words, W_wts_scales, b_wts, out):
             nc.scalar.copy(out=parts_t[:], in_=parts_ps[:])
             return parts_t
 
-        def bias_term(q, parts_t):
+        def bias_matmul(q, parts_t):
             bias_ps = psum_small.tile([P, QUAD, OUTS], F32, tag="small")
-            bias_sb = stage.tile([P, QUAD, OUTS], F32)
             nc.tensor.matmul(
                 bias_ps[:].rearrange("p i o -> p (i o)"),
                 lhsT=parts_t[:],
@@ -217,13 +227,18 @@ def tile_vclinear_t_e_kernel(tc, inputs, W_wts_words, W_wts_scales, b_wts, out):
                 start=True,
                 stop=True,
             )
-            nc.scalar.copy(out=bias_sb[:], in_=bias_ps[:])
+            bias_ps_of[q] = bias_ps
+
+        def bias_copy(q):
+            bias_sb = stage.tile([P, QUAD, OUTS], F32)
+            nc.scalar.copy(out=bias_sb[:], in_=bias_ps_of[q][:])
             for i in range(QUAD):
                 bias_of[QUAD * q + i] = bias_sb[:, i, :]
 
-        def multiply(n, x_codes, x_scales):
+        def multiply(n):
+            x_codes, x_scales = quantised_of[n]
             for h in range(BANKS):
-                prod = psum_prod.tile([P, PAIR, BANK_TERMS, OUTS], F32)
+                prod = psum.tile([P, PAIR, BANK_TERMS, OUTS], F32, tag="bank")
                 cols = slice(h * N_MOVE, (h + 1) * N_MOVE)
                 for i in range(PAIR):
                     for g in range(PASSES):
@@ -252,10 +267,10 @@ def tile_vclinear_t_e_kernel(tc, inputs, W_wts_words, W_wts_scales, b_wts, out):
                     scale=basis[:, j, 1:2],
                 )
 
-        def add_terms(n, h):
-            for i in range(PAIR):
-                j = PAIR * n + i
-                for c in range(BANK_TERMS):
+        def add_terms(n, h, sums=(0, 1)):
+            for c in sums:
+                for i in range(PAIR):
+                    j = PAIR * n + i
                     total = partial[:, c, j, :]
                     if h > 1:
                         before = total
@@ -286,32 +301,60 @@ def tile_vclinear_t_e_kernel(tc, inputs, W_wts_words, W_wts_scales, b_wts, out):
             )
             nc.sync.dma_start(out=out_dram[:, slots, :], in_=out_rows[:, slots, :])
 
-        sort_pair(0)
-        transpose_features(0)
-        parts_t = transpose_basis(0)
-        sort_pair(1)
-        transpose_features(1)
-        bias_term(0, parts_t)
-        quantised = quantise(0)
-        for n in range(N_PAIRS):
-            multiply(n, *quantised)
-            scalar_terms(n)
-            if n == 0:
-                sort_pair(2)
-            if n + 1 < N_PAIRS:
-                quantised = quantise(n + 1)
-            next_quad = (n + 1) // PAIR
-            opens_quad = n % PAIR == 1 and next_quad < N_QUADS
-            if opens_quad:
-                parts_t = transpose_basis(next_quad)
-            if n + 2 < N_PAIRS:
-                transpose_features(n + 2)
-            if opens_quad:
-                bias_term(next_quad, parts_t)
-            if n + 3 < N_PAIRS:
-                sort_pair(n + 3)
+        def finish_last_pair(n):
+            slots = slice(PAIR * n, PAIR * (n + 1))
+            add_terms(n, 1)
+            nc.vector.tensor_add(
+                out=partial[:, 0, slots, :],
+                in0=partial[:, 0, slots, :],
+                in1=second_term[:, slots, :],
+            )
+            add_terms(n, 2, sums=(1, 0))
+            add_terms(n, 3, sums=(1, 0))
+            for i in range(PAIR):
+                j = PAIR * n + i
+                nc.vector.tensor_add(
+                    out=out_rows[:, j, :], in0=partial[:, 0, j, :], in1=partial[:, 1, j, :]
+                )
+                nc.sync.dma_start(out=out_dram[:, j, :], in_=out_rows[:, j, :])
+
+        def add_all_terms(n):
             for h in range(1, BANKS):
                 add_terms(n, h)
-            if n >= 1:
-                store(n - 1)
-        store(N_PAIRS - 1)
+
+        for k in range(N_QUADS):
+            first = PAIR * k
+            slots = list(range(QUAD * k, QUAD * (k + 1)))
+            if k > 0:
+                parts_t = transpose_basis(k)
+            for j in slots:
+                transpose_slot(j)
+            for j in slots[:-1]:
+                group_slot(j)
+            if k == 0:
+                quantise(first)
+                group_slot(slots[-1])
+                parts_t = transpose_basis(k)
+            bias_matmul(k, parts_t)
+            if k > 0:
+                multiply(first - 1)
+                scalar_terms(first - 1)
+                group_slot(slots[-1])
+            bias_copy(k)
+            if k > 0:
+                quantise(first)
+            multiply(first)
+            if k > 0:
+                add_all_terms(first - 1)
+            scalar_terms(first)
+            quantise(first + 1)
+            if k + 1 < N_QUADS:
+                sort_pair(first + 2)
+                sort_pair(first + 3)
+            if k > 0:
+                store(first - 1)
+            add_all_terms(first)
+            store(first)
+        multiply(N_PAIRS - 1)
+        scalar_terms(N_PAIRS - 1)
+        finish_last_pair(N_PAIRS - 1)

@@ -37,6 +37,7 @@ PARTS = 3
 HEAD_SLOTS = 2 * QUAD
 PSUM_BANKS = 8
 ROTATING_BANKS = PSUM_BANKS - 1
+W_LOADS = 2
 FIRST_SHARED_SORT = 5
 
 
@@ -98,11 +99,16 @@ def tile_vclinear_t_e_kernel(tc, inputs, W_wts_words, W_wts_scales, b_wts, out):
             .bitcast(I32)
             .rearrange("(s g) p n -> g p s n", g=PASSES)
         )
-        for g in range(PASSES):
-            nc.sync.dma_start(
-                out=w_codes[:, g, :].bitcast(I32).rearrange("p (s n) -> p s n", s=TERMS),
-                in_=words_dram[g],
-            )
+        for half in range(W_LOADS):
+            some = slice(half * TERMS // W_LOADS, (half + 1) * TERMS // W_LOADS)
+            cols = slice(some.start * OUTS, some.stop * OUTS)
+            for g in range(PASSES):
+                nc.sync.dma_start(
+                    out=w_codes[:, g, cols]
+                    .bitcast(I32)
+                    .rearrange("p (s n) -> p s n", s=TERMS // W_LOADS),
+                    in_=words_dram[g][:, some, :],
+                )
         for i in range(QUAD):
             rows = slice(PARTS * TERMS * i, PARTS * TERMS * (i + 1))
             nc.scalar.dma_start(
@@ -329,12 +335,16 @@ def tile_vclinear_t_e_kernel(tc, inputs, W_wts_words, W_wts_scales, b_wts, out):
                 parts_t = transpose_basis(k)
             for j in slots:
                 transpose_slot(j)
-            for j in slots[:-1]:
-                group_slot(j)
             if k == 0:
+                for j in slots[:PAIR]:
+                    group_slot(j)
                 quantise(first)
-                group_slot(slots[-1])
                 parts_t = transpose_basis(k)
+                for j in slots[PAIR:]:
+                    group_slot(j)
+            else:
+                for j in slots[:-1]:
+                    group_slot(j)
             bias_matmul(k, parts_t)
             if k > 0:
                 multiply(first - 1)

@@ -78,12 +78,13 @@ def tile_vclinear_t_e_kernel(tc, inputs, W_wts_words, W_wts_scales, b_wts, out):
             slots = slice(PAIR * n, PAIR * (n + 1))
             nc.sync.dma_start(out=x_rows[:, slots, :], in_=rows_dram[:, slots, 1:])
 
-        def load_treatments(first, last):
-            nc.sync.dma_start(
+        def load_treatments(queue, first, last):
+            queue.dma_start(
                 out=t_rows[:, first:last, :], in_=rows_dram[:, first:last, 0:T_PIECE]
             )
 
-        load_treatments(0, HEAD_SLOTS)
+        load_treatments(nc.sync, 0, HEAD_SLOTS)
+        load_treatments(nc.scalar, HEAD_SLOTS, SLOTS)
         load_pair(0)
         load_pair(1)
         scales_dram = W_wts_scales.bitcast(I32).rearrange("m (a r) n -> a r m n", r=4)
@@ -115,7 +116,6 @@ def tile_vclinear_t_e_kernel(tc, inputs, W_wts_words, W_wts_scales, b_wts, out):
                 out=bias_w[rows, i, :],
                 in_=b_wts.unsqueeze(0).to_broadcast([PARTS, TERMS, OUTS]),
             )
-        load_treatments(HEAD_SLOTS, SLOTS)
         for n in range(2, N_PAIRS):
             load_pair(n)
 

@@ -32,6 +32,7 @@ N_MOVE = BANK_TERMS * OUTS
 BANKS = TERMS // BANK_TERMS
 BANK_COLS = PAIR * N_MOVE
 T_PIECE = 2
+T_PITCH = 16
 SUMS = 2
 PARTS = 3
 HEAD_SLOTS = 2 * QUAD
@@ -54,7 +55,7 @@ def tile_vclinear_t_e_kernel(tc, inputs, W_wts_words, W_wts_scales, b_wts, out):
         ident = keep.tile([P, P], F32)
         ident_bf = keep.tile([P, P], BF16)
         x_rows = keep.tile([P, SLOTS, FEATURES], BF16, align_bytes=64)
-        t_rows = keep.tile([P, SLOTS, T_PIECE], BF16)
+        t_rows = keep.tile([P, SLOTS, T_PITCH], BF16)
         w_codes = keep.tile([P, PASSES, TERMS * OUTS], U32, align_bytes=64)
         w_scales = keep.tile([P, PASSES, TERMS * OUTS], U8, align_bytes=64)
         scale_rows = keep.tile([P, TERMS * PASSES * OUTS], U8, align_bytes=64)
@@ -80,7 +81,7 @@ def tile_vclinear_t_e_kernel(tc, inputs, W_wts_words, W_wts_scales, b_wts, out):
 
         def load_treatments(queue, first, last):
             queue.dma_start(
-                out=t_rows[:, first:last, :], in_=rows_dram[:, first:last, 0:T_PIECE]
+                out=t_rows[:, first:last, 0:T_PIECE], in_=rows_dram[:, first:last, 0:T_PIECE]
             )
 
         load_treatments(nc.sync, 0, HEAD_SLOTS)

@@ -84,8 +84,8 @@ def tile_vclinear_t_e_kernel(tc, inputs, W_wts_words, W_wts_scales, b_wts, out):
                 out=t_rows[:, first:last, 0:T_PIECE], in_=rows_dram[:, first:last, 0:T_PIECE]
             )
 
-        load_treatments(nc.sync, 0, HEAD_SLOTS)
-        load_treatments(nc.scalar, HEAD_SLOTS, SLOTS)
+        load_treatments(nc.scalar, 0, HEAD_SLOTS)
+        load_treatments(nc.gpsimd, HEAD_SLOTS, SLOTS)
         load_pair(0)
         load_pair(1)
         scales_dram = W_wts_scales.bitcast(I32).rearrange("m (a r) n -> a r m n", r=4)

@@ -359,7 +359,7 @@ def tile_vclinear_t_e_kernel(tc, inputs, W_wts_words, W_wts_scales, b_wts, out):
                 add_all_terms(first - 1)
             scalar_terms(first)
             quantise(first + 1)
-            if k + 1 < N_QUADS:
+            if 0 < k < N_QUADS - 1:
                 sort_pair(first + 2)
                 sort_pair(first + 3)
             if k > 0:

from contextlib import ExitStack

import concourse.mybir as mybir
from concourse.masks import make_identity

F32 = mybir.dt.float32
BF16 = mybir.dt.bfloat16
I32 = mybir.dt.int32
U32 = mybir.dt.uint32
U8 = mybir.dt.uint8
FP8X4 = mybir.dt.float8_e4m3fn_x4
ALU = mybir.AluOpType
ACT = mybir.ActivationFunctionType

P = 128
BATCH, FEATURES, OUTS, TERMS = 4096, 1024, 128, 8
KNOTS = (0.2, 0.4, 0.6, 0.8)
FLOPS = 2 * BATCH * FEATURES * TERMS * OUTS

PACK = 4
K_PASS = P * PACK
PASSES = FEATURES // K_PASS
HALF_WORDS = 2

SLOTS = BATCH // P
PAIR = 2
N_PAIRS = SLOTS // PAIR
QUAD = 4
N_QUADS = SLOTS // QUAD
BANK_TERMS = 2
N_MOVE = BANK_TERMS * OUTS
BANKS = TERMS // BANK_TERMS
BANK_COLS = PAIR * N_MOVE
T_PIECE = 2
T_PITCH = 16
SUMS = 2
PARTS = 3
HEAD_SLOTS = 2 * QUAD
PSUM_BANKS = 8
ROTATING_BANKS = PSUM_BANKS - 1
W_LOADS = 2
FIRST_SHARED_SORT = 5


def tile_vclinear_t_e_kernel(tc, inputs, W_wts_words, W_wts_scales, b_wts, out):
    nc = tc.nc
    with ExitStack() as ctx:
        ctx.enter_context(tc.manual_schedule())
        keep = ctx.enter_context(tc.tile_pool(name="keep", bufs=1))
        stage = ctx.enter_context(tc.tile_pool(name="stage", bufs=3))
        sorted_pool = ctx.enter_context(tc.tile_pool(name="sorted", bufs=4 * PAIR))
        psum = ctx.enter_context(tc.psum_pool(name="psum", bufs=ROTATING_BANKS))
        psum_small = ctx.enter_context(tc.psum_pool(name="psum_small", bufs=1))

        ident = keep.tile([P, P], F32)
        ident_bf = keep.tile([P, P], BF16)
        x_rows = keep.tile([P, SLOTS, FEATURES], BF16, align_bytes=64)
        t_rows = keep.tile([P, SLOTS, T_PITCH], BF16)
        w_codes = keep.tile([P, PASSES, TERMS * OUTS], U32, align_bytes=64)
        w_scales = keep.tile([P, PASSES, TERMS * OUTS], U8, align_bytes=64)
        scale_rows = keep.tile([P, TERMS * PASSES * OUTS], U8, align_bytes=64)
        bias_w = keep.tile([P, QUAD, OUTS], BF16)
        basis = keep.tile([P, SLOTS, TERMS], F32)
        basis_parts = keep.tile([P, N_QUADS, P], BF16)
        first_product = keep.tile([P, SLOTS, OUTS], F32)
        second_term = keep.tile([P, SLOTS, OUTS], F32)
        partial = keep.tile([P, SUMS, SLOTS, OUTS], F32)
        out_rows = keep.tile([P, SLOTS, OUTS], F32)

        make_identity(nc, ident[:])
        make_identity(nc, ident_bf[:])
        nc.vector.memset(scale_rows[:].bitcast(I32), 0)
        nc.vector.memset(bias_w[:], 0.0)
        nc.vector.memset(basis_parts[:], 0.0)

        rows_dram = inputs.rearrange("(p j) c -> p j c", j=SLOTS)

        def load_pair(n):
            slots = slice(PAIR * n, PAIR * (n + 1))
            nc.sync.dma_start(out=x_rows[:, slots, :], in_=rows_dram[:, slots, 1:])

        def load_treatments(queue, first, last):
            queue.dma_start(
                out=t_rows[:, first:last, 0:T_PIECE], in_=rows_dram[:, first:last, 0:T_PIECE]
            )

        load_treatments(nc.scalar, 0, HEAD_SLOTS)
        load_treatments(nc.gpsimd, HEAD_SLOTS, SLOTS)
        load_pair(0)
        load_pair(1)
        scales_dram = W_wts_scales.bitcast(I32).rearrange("m (a r) n -> a r m n", r=4)
        for a in range(4):
            nc.sync.dma_start(
                out=scale_rows[32 * a : 32 * a + 4, :]
                .bitcast(I32)
                .rearrange("r (m n) -> r m n", m=TERMS * PASSES),
                in_=scales_dram[a],
            )
        words_dram = (
            W_wts_words.rearrange("m p n t -> m p (n t)")
            .bitcast(I32)
            .rearrange("(s g) p n -> g p s n", g=PASSES)
        )
        for half in range(W_LOADS):
            some = slice(half * TERMS // W_LOADS, (half + 1) * TERMS // W_LOADS)
            cols = slice(some.start * OUTS, some.stop * OUTS)
            for g in range(PASSES):
                nc.sync.dma_start(
                    out=w_codes[:, g, cols]
                    .bitcast(I32)
                    .rearrange("p (s n) -> p s n", s=TERMS // W_LOADS),
                    in_=words_dram[g][:, some, :],
                )
        for i in range(QUAD):
            rows = slice(PARTS * TERMS * i, PARTS * TERMS * (i + 1))
            nc.scalar.dma_start(
                out=bias_w[rows, i, :],
                in_=b_wts.unsqueeze(0).to_broadcast([PARTS, TERMS, OUTS]),
            )
        for n in range(2, N_PAIRS):
            load_pair(n)

        def spline_basis(engine, first, last):
            count = last - first
            slots = slice(first, last)
            fn = basis[:, slots, :]
            hinge = keep.tile([P, count, len(KNOTS)], F32, name="hinge_%d" % first)
            hinge_sq = keep.tile([P, count, len(KNOTS)], F32, name="hinge_sq_%d" % first)
            rest = keep.tile([P, count, TERMS], F32, name="rest_%d" % first)
            engine.memset(fn[:, :, 0], 1.0)
            engine.tensor_copy(out=fn[:, :, 1], in_=t_rows[:, slots, 0])
            engine.tensor_mul(out=fn[:, :, 2], in0=fn[:, :, 1], in1=fn[:, :, 1])
            engine.tensor_mul(out=fn[:, :, 3], in0=fn[:, :, 2], in1=fn[:, :, 1])
            for c, knot in enumerate(KNOTS):
                engine.tensor_scalar(
                    out=hinge[:, :, c],
                    in0=fn[:, :, 1],
                    scalar1=knot,
                    scalar2=0.0,
                    op0=ALU.subtract,
                    op1=ALU.max,
                )
            engine.tensor_mul(out=hinge_sq[:], in0=hinge[:], in1=hinge[:])
            engine.tensor_mul(out=fn[:, :, 4:TERMS], in0=hinge_sq[:], in1=hinge[:])
            part = basis_parts[:, first // QUAD : last // QUAD, 0 : QUAD * PARTS * TERMS].rearrange(
                "p q (i r s) -> p q i r s", i=QUAD, r=PARTS
            )
            fn_q = fn.rearrange("p (q i) s -> p q i s", i=QUAD)
            rest_q = rest[:].rearrange("p (q i) s -> p q i s", i=QUAD)
            engine.tensor_copy(out=part[:, :, :, 0, :], in_=fn_q)
            engine.tensor_sub(out=rest_q, in0=fn_q, in1=part[:, :, :, 0, :])
            engine.tensor_copy(out=part[:, :, :, 1, :], in_=rest_q)
            engine.tensor_sub(out=part[:, :, :, 2, :], in0=rest_q, in1=part[:, :, :, 1, :])

        spline_basis(nc.vector, 0, HEAD_SLOTS)

        nc.gpsimd.tensor_copy(
            out=w_scales[:]
            .rearrange("p g c -> p (g c)")
            .bitcast(I32)
            .rearrange("p (g s n) -> p g s n", g=PASSES, s=TERMS),
            in_=scale_rows[:].bitcast(I32).rearrange("p (s g n) -> p g s n", g=PASSES, s=TERMS),
        )
        spline_basis(nc.gpsimd, HEAD_SLOTS, SLOTS)

        halves_of = {}
        xt_of = {}
        grouped_of = {}
        quantised_of = {}
        bias_ps_of = {}
        products = {}
        bias_of = {}

        def sort_words(j, on_gpsimd):
            halves = sorted_pool.tile([P, PASSES, HALF_WORDS, P], F32)
            words = x_rows[:, j, :].bitcast(F32)
            source = words.rearrange("p (g c u) -> p g u c", g=PASSES, u=HALF_WORDS)
            if on_gpsimd:
                nc.gpsimd.tensor_copy(out=halves[:], in_=source)
            else:
                nc.scalar.copy(out=halves[:], in_=source)
            halves_of[j] = halves

        def sort_pair(n):
            sort_words(PAIR * n, False)
            sort_words(PAIR * n + 1, n >= FIRST_SHARED_SORT)

        def transpose_slot(j):
            xt = psum.tile([P, PASSES, HALF_WORDS, P], F32, tag="bank")
            words = x_rows[:, j, :].bitcast(F32)
            for g in range(PASSES):
                for u in range(HALF_WORDS):
                    if j in halves_of:
                        source = halves_of[j][:, g, u, :]
                    else:
                        first_word = g * HALF_WORDS * P + u
                        source = words[:, first_word : (g + 1) * HALF_WORDS * P : HALF_WORDS]
                    nc.tensor.transpose(xt[:, g, u, :], source, ident[:])
            xt_of[j] = xt

        def group_slot(j):
            n, i = divmod(j, PAIR)
            if i == 0:
                grouped = stage.tile([P, PAIR, PASSES, P, PACK], BF16, align_bytes=64)
                grouped_of[n] = grouped
            nc.scalar.copy(
                out=grouped_of[n][:, i].bitcast(F32),
                in_=xt_of[j][:].rearrange("p g u b -> p g b u"),
            )

        def quantise(n):
            x_codes = stage.tile([P, PAIR * PASSES * P], U32, align_bytes=64)
            x_scales = stage.tile([P, PAIR * PASSES * P], U8, align_bytes=64)
            nc.vector.quantize_mx(
                out=x_codes[:].bitcast(FP8X4),
                scales=x_scales[:],
                in_=grouped_of[n][:].rearrange("p i g b t -> p (i g b t)"),
            )
            quantised_of[n] = (x_codes, x_scales)

        def transpose_basis(q):
            parts_ps = psum_small.tile([P, P], BF16, tag="small")
            parts_t = stage.tile([P, P], BF16)
            nc.tensor.transpose(parts_ps[:], basis_parts[:, q, :], ident_bf[:])
            nc.scalar.copy(out=parts_t[:], in_=parts_ps[:])
            return parts_t

        def bias_matmul(q, parts_t):
            bias_ps = psum_small.tile([P, QUAD, OUTS], F32, tag="small")
            nc.tensor.matmul(
                bias_ps[:].rearrange("p i o -> p (i o)"),
                lhsT=parts_t[:],
                rhs=bias_w[:].rearrange("p i o -> p (i o)"),
                start=True,
                stop=True,
            )
            bias_ps_of[q] = bias_ps

        def bias_copy(q):
            bias_sb = stage.tile([P, QUAD, OUTS], F32)
            nc.scalar.copy(out=bias_sb[:], in_=bias_ps_of[q][:])
            for i in range(QUAD):
                bias_of[QUAD * q + i] = bias_sb[:, i, :]

        def multiply(n):
            x_codes, x_scales = quantised_of[n]
            for h in range(BANKS):
                prod = psum.tile([P, PAIR, BANK_TERMS, OUTS], F32, tag="bank")
                cols = slice(h * N_MOVE, (h + 1) * N_MOVE)
                for i in range(PAIR):
                    for g in range(PASSES):
                        rows = slice((i * PASSES + g) * P, (i * PASSES + g + 1) * P)
                        nc.tensor.matmul_mx(
                            out=prod[:, i].rearrange("p s o -> p (s o)"),
                            lhsT=x_codes[:, rows].bitcast(FP8X4),
                            lhsT_scale=x_scales[:, rows],
                            rhs=w_codes[:, g, cols].bitcast(FP8X4),
                            rhs_scale=w_scales[:, g, cols],
                            start=(g == 0),
                            stop=(g == PASSES - 1),
                        )
                products[(n, h)] = prod

        def scalar_terms(n):
            slots = slice(PAIR * n, PAIR * (n + 1))
            prod = products[(n, 0)]
            nc.scalar.copy(out=first_product[:, slots, :], in_=prod[:, :, 0, :])
            for i in range(PAIR):
                j = PAIR * n + i
                nc.scalar.activation(
                    out=second_term[:, j, :],
                    in_=prod[:, i, 1, :],
                    func=ACT.Copy,
                    scale=basis[:, j, 1:2],
                )

        def add_terms(n, h, sums=(0, 1)):
            for c in sums:
                for i in range(PAIR):
                    j = PAIR * n + i
                    total = partial[:, c, j, :]
                    if h > 1:
                        before = total
                    elif c == 0:
                        before = bias_of[j]
                    else:
                        before = first_product[:, j, :]
                    s = BANK_TERMS * h + c
                    nc.vector.scalar_tensor_tensor(
                        out=total,
                        in0=products[(n, h)][:, i, c, :],
                        scalar=basis[:, j, s : s + 1],
                        in1=before,
                        op0=ALU.mult,
                        op1=ALU.add,
                    )

        out_dram = out.rearrange("(p j) o -> p j o", j=SLOTS)

        def store(n):
            slots = slice(PAIR * n, PAIR * (n + 1))
            both = stage.tile([P, PAIR, OUTS], F32)
            nc.gpsimd.tensor_add(
                out=both[:], in0=partial[:, 0, slots, :], in1=partial[:, 1, slots, :]
            )
            nc.gpsimd.tensor_add(
                out=out_rows[:, slots, :], in0=both[:], in1=second_term[:, slots, :]
            )
            nc.sync.dma_start(out=out_dram[:, slots, :], in_=out_rows[:, slots, :])

        def finish_last_pair(n):
            slots = slice(PAIR * n, PAIR * (n + 1))
            add_terms(n, 1)
            nc.vector.tensor_add(
                out=partial[:, 0, slots, :],
                in0=partial[:, 0, slots, :],
                in1=second_term[:, slots, :],
            )
            add_terms(n, 2, sums=(1, 0))
            add_terms(n, 3, sums=(1, 0))
            for i in range(PAIR):
                j = PAIR * n + i
                nc.vector.tensor_add(
                    out=out_rows[:, j, :], in0=partial[:, 0, j, :], in1=partial[:, 1, j, :]
                )
                nc.sync.dma_start(out=out_dram[:, j, :], in_=out_rows[:, j, :])

        def add_all_terms(n):
            for h in range(1, BANKS):
                add_terms(n, h)

        for k in range(N_QUADS):
            first = PAIR * k
            slots = list(range(QUAD * k, QUAD * (k + 1)))
            if k > 0:
                parts_t = transpose_basis(k)
            for j in slots:
                transpose_slot(j)
            if k == 0:
                for j in slots[:PAIR]:
                    group_slot(j)
                quantise(first)
                parts_t = transpose_basis(k)
                for j in slots[PAIR:]:
                    group_slot(j)
            else:
                for j in slots[:-1]:
                    group_slot(j)
            bias_matmul(k, parts_t)
            if k > 0:
                multiply(first - 1)
                scalar_terms(first - 1)
                group_slot(slots[-1])
            bias_copy(k)
            if k > 0:
                quantise(first)
            multiply(first)
            if k > 0:
                add_all_terms(first - 1)
            scalar_terms(first)
            quantise(first + 1)
            if 0 < k < N_QUADS - 1:
                sort_pair(first + 2)
                sort_pair(first + 3)
            if k > 0:
                store(first - 1)
            add_all_terms(first)
            store(first)
        multiply(N_PAIRS - 1)
        scalar_terms(N_PAIRS - 1)
        finish_last_pair(N_PAIRS - 1)
